import numpy as np
import ml_dtypes


def mxq(x, axis, fmt="e4m3"):
    dtype, down = {"e4m3": (ml_dtypes.float8_e4m3fn, 7), "e5m2": (ml_dtypes.float8_e5m2, 14)}[fmt]
    v = np.moveaxis(np.asarray(x, np.float32).astype(ml_dtypes.bfloat16).astype(np.float64), axis, -1)
    blocks = v.reshape(v.shape[:-1] + (-1, 32))
    amax = np.abs(blocks).max(-1, keepdims=True)
    byte = np.maximum(np.where(amax > 0, np.frexp(amax)[1] - 1 + 127, 0) - down, 1)
    scale = np.exp2(byte - 127.0)
    codes = (blocks / scale).astype(np.float32).astype(dtype).astype(np.float64)
    return np.moveaxis((codes * scale).reshape(v.shape), -1, axis)


WIDE = False


def mx_kscale(k):
    if not WIDE:
        return np.ones(k)
    levels = np.array([10, -10, 5, -5, 0])
    a = np.random.permutation(np.resize(levels, k // 512 * 4)).reshape(k // 512, 4)
    idx = np.arange(k)
    return np.exp2(a[idx // 512, idx % 128 // 32])


BF16 = ml_dtypes.bfloat16


def bf(x):
    return np.asarray(x, np.float32).astype(BF16)


def f64(x):
    return np.asarray(x).astype(np.float64)


B, Q, P, H1, H2, C, GN, KO = 1024, 7, 4, 512, 512, 256, 10, 3
NB = GN + KO
LO, HI = -2.0, 2.0


def mish(v):
    return v * np.tanh(np.logaddexp(0.0, v))


def bspline_basis(v):
    step = (HI - LO) / GN
    knots = LO + step * np.arange(-KO, GN + KO + 1)
    vv = v[..., None]
    bas = np.where((vv >= knots[:-1]) & (vv < knots[1:]), 1.0, 0.0)
    for d in range(1, KO + 1):
        left = (vv - knots[: -(d + 1)]) / (knots[d:-1] - knots[: -(d + 1)]) * bas[..., :-1]
        right = (knots[d + 1:] - vv) / (knots[d + 1:] - knots[1:-d]) * bas[..., 1:]
        bas = left + right
    return bas


def setup_inputs():
    t = np.minimum(mx_kscale(H1), 1.0) ** 2
    return {'h1': bf(np.random.standard_normal((B, H1)) * t),
            'coef2': bf(np.random.standard_normal((H1, H2, NB)) / np.sqrt(H1)),
            'sb2': bf(np.random.standard_normal((H1, H2)) / np.sqrt(H1) / t[:, None]),
            'sp2': bf(1.0 + 0.3 * np.random.standard_normal((H1, H2))),
            'b2': bf(0.2 * np.random.standard_normal(H2))}


def reference(h1, coef2, sb2, sp2, b2):
    x = f64(h1)
    phi = bspline_basis(x).transpose(2, 0, 1)
    w = (f64(coef2) * f64(sp2)[..., None]).transpose(2, 0, 1)
    spline = (mxq(phi, 2, 'e4m3') @ mxq(w, 1, 'e4m3')).sum(0)
    base = mxq(mish(x), 1, 'e4m3') @ mxq(f64(sb2), 0, 'e4m3')
    return base + spline + f64(b2)

@@ -1,0 +1,246 @@
+import math
+
+import concourse.masks as masks
+import concourse.mybir as mybir
+
+F32 = mybir.dt.float32
+BF16 = mybir.dt.bfloat16
+U32 = mybir.dt.uint32
+U8 = mybir.dt.uint8
+FP8X4 = mybir.dt.float8_e4m3fn_x4
+ALU = mybir.AluOpType
+ACT = mybir.ActivationFunctionType
+
+P = 128
+PACK = 4
+BATCH, FEATURES, OUTPUTS, BASIS = 1024, 512, 512, 13
+COMBS = 4
+BRANCHES = BASIS + 1
+MISH = BASIS
+FLOPS = 2 * BATCH * OUTPUTS * FEATURES * BRANCHES
+
+ROW_TILES = BATCH // P
+TILES_PER_CHUNK = 2
+CHUNKS = ROW_TILES // TILES_PER_CHUNK
+CHUNK_WORDS = TILES_PER_CHUNK * P
+CHUNK = CHUNK_WORDS * PACK
+ALL = CHUNKS * CHUNK
+
+O_PIECE = 128
+O_PIECES = OUTPUTS // O_PIECE
+G_RUN = 4
+
+ROUND = 12582912.0
+V_EDGE = 3.25
+V_CAP = 20.0
+ROOT_SIXTH = math.sqrt(1.0 / 6.0)
+ROOT_TWO_THIRDS = math.sqrt(2.0 / 3.0)
+
+
+def half_of_features(matrix, u):
+    half = FEATURES // 2
+    return matrix[u * half : (u + 1) * half]
+
+
+def tile_net_pa_kernel(tc, h1, coef2, sb2, sp2, b2, out):
+    nc = tc.nc
+    with (
+        tc.tile_pool(name="keep", bufs=1) as keep,
+        tc.tile_pool(name="work", bufs=1) as work,
+        tc.tile_pool(name="ring", bufs=2) as ring,
+        tc.psum_pool(name="psum", bufs=2) as psum,
+    ):
+        h1_rows = work.tile([P, ROW_TILES, FEATURES], BF16, tag="early")
+        h1_by_tile = h1.rearrange("(m p) i -> p m i", p=P)
+        for c in range(CHUNKS):
+            tiles = slice(c * TILES_PER_CHUNK, (c + 1) * TILES_PER_CHUNK)
+            nc.sync.dma_start(out=h1_rows[:, tiles, :], in_=h1_by_tile[:, tiles, :])
+        gain = keep.tile([P, PACK, OUTPUTS], BF16)
+        base_raw = keep.tile([P, PACK, OUTPUTS], BF16)
+        for u in range(2):
+            nc.sync.dma_start(
+                out=gain[:, 2 * u : 2 * u + 2, :],
+                in_=half_of_features(sp2, u).rearrange("(p e) o -> p e o", e=2),
+            )
+
+        def load_coef(piece):
+            coef_raw = ring.tile([P, PACK, O_PIECE * BASIS], BF16)
+            columns = slice(piece * O_PIECE, (piece + 1) * O_PIECE)
+            for u in range(2):
+                nc.sync.dma_start(
+                    out=coef_raw[:, 2 * u : 2 * u + 2, :],
+                    in_=half_of_features(coef2, u)[:, columns, :].rearrange("(p e) o g -> p e (o g)", e=2),
+                )
+            return coef_raw
+
+        coef_pieces = [load_coef(0), load_coef(1)]
+        for u in range(2):
+            nc.sync.dma_start(
+                out=base_raw[:, 2 * u : 2 * u + 2, :],
+                in_=half_of_features(sb2, u).rearrange("(p e) o -> p e o", e=2),
+            )
+        bias = keep.tile([P, OUTPUTS], BF16)
+        nc.sync.dma_start(out=bias[:], in_=b2.partition_broadcast(P))
+
+        identity = keep.tile([P, P], F32)
+        masks.make_identity(nc, identity[:])
+        h1_words = h1_rows[:].bitcast(F32)
+        v = keep.tile([P, ALL], BF16, align_bytes=64)
+        v_words = v[:].bitcast(F32).rearrange("p (c m b u) -> p c m b u", c=CHUNKS, m=TILES_PER_CHUNK, u=2)
+        for c in range(CHUNKS):
+            turned = psum.tile([P, TILES_PER_CHUNK, 2, P], F32)
+            for m in range(TILES_PER_CHUNK):
+                for u in range(2):
+                    nc.tensor.transpose(
+                        out=turned[:, m, u, :],
+                        in_=h1_words[:, c * TILES_PER_CHUNK + m, u * P : (u + 1) * P],
+                        identity=identity[:],
+                    )
+            nc.scalar.copy(out=v_words[:, c], in_=turned[:].rearrange("p m u b -> p m b u"))
+
+        v_capped = work.tile([P, ALL], BF16, tag="early")
+        nc.vector.tensor_scalar_min(out=v_capped[:], in0=v[:], scalar1=V_CAP)
+        v_clipped = keep.tile([P, ALL], BF16)
+        nc.vector.tensor_scalar(
+            out=v_clipped[:], in0=v[:], scalar1=-V_EDGE, scalar2=V_EDGE, op0=ALU.max, op1=ALU.min
+        )
+        gate = work.tile([P, ALL], F32, tag="wide")
+        nc.scalar.activation(out=gate[:], in_=v_capped[:], func=ACT.Exp)
+        nc.scalar.activation(out=gate[:], in_=gate[:], func=ACT.Ln, bias=1.0)
+        nc.scalar.activation(out=gate[:], in_=gate[:], func=ACT.Tanh)
+
+        w_codes = keep.tile([P, BRANCHES, OUTPUTS], U32, align_bytes=64)
+        w_scales = keep.tile([P, BRANCHES, OUTPUTS], U8, align_bytes=64)
+        for piece in range(O_PIECES):
+            columns = slice(piece * O_PIECE, (piece + 1) * O_PIECE)
+            coef = coef_pieces[piece][:].rearrange("p t (o g) -> p t o g", g=BASIS)
+            w_grouped = work.tile([P, BASIS, O_PIECE, PACK], BF16, align_bytes=64)
+            for g0 in range(0, BASIS, G_RUN):
+                g_run = slice(g0, min(g0 + G_RUN, BASIS))
+                count = min(G_RUN, BASIS - g0)
+                nc.vector.tensor_tensor(
+                    out=w_grouped[:, g_run].rearrange("p g o t -> p o t g"),
+                    in0=coef[:, :, :, g_run].rearrange("p t o g -> p o t g"),
+                    in1=gain[:, :, columns]
+                    .rearrange("p t o -> p o t")
+                    .unsqueeze(3)
+                    .to_broadcast([P, O_PIECE, PACK, count]),
+                    op=ALU.mult,
+                )
+            if piece + 2 < O_PIECES:
+                coef_pieces.append(load_coef(piece + 2))
+            for g in range(BASIS):
+                nc.vector.quantize_mx(
+                    out=w_codes[:, g, columns].bitcast(FP8X4),
+                    scales=w_scales[:, g, columns],
+                    in_=w_grouped[:, g].rearrange("p o t -> p (o t)"),
+                )
+        base_grouped = work.tile([P, OUTPUTS, PACK], BF16, tag="slabs", align_bytes=64)
+        nc.vector.tensor_copy(out=base_grouped[:], in_=base_raw[:].rearrange("p t o -> p o t"))
+        nc.vector.quantize_mx(
+            out=w_codes[:, MISH, :].bitcast(FP8X4),
+            scales=w_scales[:, MISH, :],
+            in_=base_grouped[:].rearrange("p o t -> p (o t)"),
+        )
+
+        mish = work.tile([P, ALL], BF16, tag="slabs", align_bytes=64)
+        nc.vector.tensor_tensor(out=mish[:], in0=v[:], in1=gate[:], op=ALU.mult)
+        mish_codes = keep.tile([P, ALL // PACK], U32, align_bytes=64)
+        mish_scales = keep.tile([P, ALL // PACK], U8, align_bytes=64)
+        nc.vector.quantize_mx(out=mish_codes[:].bitcast(FP8X4), scales=mish_scales[:], in_=mish[:])
+
+        for c in range(CHUNKS):
+            vc = v_clipped[:, c * CHUNK : (c + 1) * CHUNK]
+            acc = [psum.tile([P, OUTPUTS], F32, name="acc", bufs=2 * TILES_PER_CHUNK) for m in range(TILES_PER_CHUNK)]
+
+            def multiply(codes, scales, branch, first, last):
+                for m in range(TILES_PER_CHUNK):
+                    rows = slice(m * P, (m + 1) * P)
+                    nc.tensor.matmul_mx(
+                        out=acc[m][:],
+                        lhsT=codes[:, rows].bitcast(FP8X4),
+                        lhsT_scale=scales[:, rows],
+                        rhs=w_codes[:, branch, :].bitcast(FP8X4),
+                        rhs_scale=w_scales[:, branch, :],
+                        start=first,
+                        stop=last,
+                    )
+
+            words = slice(c * CHUNK_WORDS, (c + 1) * CHUNK_WORDS)
+            multiply(mish_codes[:, words], mish_scales[:, words], MISH, True, False)
+
+            centred = work.tile([P, COMBS, CHUNK], F32, tag="wide")
+            for r in range(COMBS):
+                nc.scalar.activation(
+                    out=centred[:, r, :], in_=vc, func=ACT.Identity, scale=2.5 / 4.0, bias=(6.0 - r) / 4.0
+                )
+            window = work.tile([P, COMBS, CHUNK], BF16)
+            nc.vector.tensor_scalar(
+                out=window[:], in0=centred[:], scalar1=ROUND, scalar2=ROUND, op0=ALU.add, op1=ALU.subtract
+            )
+
+            beta = work.tile([P, 2, CHUNK], F32)
+            from_centre = work.tile([P, CHUNK], F32)
+            folded_0 = work.tile([P, CHUNK], F32)
+            folded_1 = work.tile([P, CHUNK], F32)
+            nc.scalar.activation(out=from_centre[:], in_=vc, func=ACT.Abs, scale=2.5)
+            nc.scalar.activation(out=folded_1[:], in_=vc, func=ACT.Abs, scale=2.5, bias=-1.0)
+            nc.scalar.activation(out=folded_0[:], in_=from_centre[:], func=ACT.Abs, bias=-6.0)
+            nc.scalar.activation(out=folded_1[:], in_=folded_1[:], func=ACT.Abs, bias=-4.0)
+            nc.scalar.activation(out=folded_0[:], in_=folded_0[:], func=ACT.Abs, bias=-2.0)
+            nc.scalar.activation(out=folded_1[:], in_=folded_1[:], func=ACT.Abs, bias=-2.0)
+            nc.vector.tensor_tensor(out=beta[:, 0, :], in0=from_centre[:], in1=folded_0[:], op=ALU.min)
+            nc.scalar.activation(out=beta[:, 1, :], in_=folded_1[:], func=ACT.Identity, scale=-1.0, bias=2.0)
+
+            near = work.tile([P, 2, CHUNK], F32)
+            far = work.tile([P, 2, CHUNK], F32)
+            kink = work.tile([P, 2, CHUNK], F32)
+            nc.scalar.activation(
+                out=kink[:], in_=beta[:], func=ACT.Square, scale=ROOT_TWO_THIRDS, bias=-ROOT_TWO_THIRDS
+            )
+            nc.scalar.activation(out=near[:], in_=beta[:], func=ACT.Square, scale=ROOT_SIXTH)
+            nc.scalar.activation(out=far[:], in_=beta[:], func=ACT.Square, scale=-ROOT_SIXTH, bias=2.0 * ROOT_SIXTH)
+            nc.vector.scalar_tensor_tensor(
+                out=kink[:], in0=beta[:], scalar=1.0, in1=kink[:], op0=ALU.subtract, op1=ALU.mult
+            )
+            nc.vector.tensor_tensor(out=near[:], in0=beta[:], in1=near[:], op=ALU.mult)
+            nc.vector.scalar_tensor_tensor(
+                out=far[:], in0=beta[:], scalar=2.0, in1=far[:], op0=ALU.subtract, op1=ALU.mult
+            )
+            periodic = work.tile([P, COMBS, CHUNK], BF16)
+            nc.vector.scalar_tensor_tensor(
+                out=periodic[:, 0:2, :], in0=kink[:], scalar=0.0, in1=near[:], op0=ALU.max, op1=ALU.subtract
+            )
+            nc.vector.scalar_tensor_tensor(
+                out=periodic[:, 2:4, :], in0=kink[:], scalar=0.0, in1=far[:], op0=ALU.min, op1=ALU.subtract
+            )
+
+            for r in range(COMBS):
+                members = list(range(r, BASIS, COMBS))
+                sign = -1.0 if r < 2 else 1.0
+                inside = work.tile([P, COMBS, CHUNK], BF16)
+                for n in range(len(members)):
+                    nc.vector.tensor_scalar(
+                        out=inside[:, n, :], in0=window[:, r, :], scalar1=float(n), scalar2=sign,
+                        op0=ALU.is_equal, op1=ALU.mult,
+                    )
+                slabs = work.tile([P, COMBS, CHUNK], BF16, tag="slabs", align_bytes=64)
+                nc.vector.tensor_tensor(
+                    out=slabs[:, 0 : len(members), :],
+                    in0=periodic[:, r : r + 1, :].to_broadcast([P, len(members), CHUNK]),
+                    in1=inside[:, 0 : len(members), :],
+                    op=ALU.mult,
+                )
+                codes = ring.tile([P, COMBS, CHUNK_WORDS], U32, align_bytes=64, bufs=3)
+                scales = ring.tile([P, COMBS, CHUNK_WORDS], U8, align_bytes=64, bufs=3)
+                for n, g in enumerate(members):
+                    nc.vector.quantize_mx(
+                        out=codes[:, n, :].bitcast(FP8X4), scales=scales[:, n, :], in_=slabs[:, n, :]
+                    )
+                    multiply(codes[:, n, :], scales[:, n, :], g, False, r == COMBS - 1 and g == members[-1])
+
+            for m in range(TILES_PER_CHUNK):
+                result = ring.tile([P, OUTPUTS], F32)
+                nc.vector.tensor_tensor(out=result[:], in0=acc[m][:], in1=bias[:], op=ALU.add)
+                row0 = (c * TILES_PER_CHUNK + m) * P
+                nc.sync.dma_start(out=out[row0 : row0 + P, :], in_=result[:])

@@ -14,10 +14,13 @@ ACT = mybir.ActivationFunctionType
 P = 128
 PACK = 4
 BATCH, FEATURES, OUTPUTS, BASIS = 1024, 512, 512, 13
-COMBS = 4
 BRANCHES = BASIS + 1
 MISH = BASIS
 FLOPS = 2 * BATCH * OUTPUTS * FEATURES * BRANCHES
+
+COMBS = 4
+WINDOWS = 4
+COMB_OF_ROW = (0, 3, 2, 1)
 
 ROW_TILES = BATCH // P
 TILES_PER_CHUNK = 2
@@ -33,8 +36,9 @@ G_RUN = 4
 ROUND = 12582912.0
 V_EDGE = 3.25
 V_CAP = 20.0
-ROOT_SIXTH = math.sqrt(1.0 / 6.0)
 ROOT_TWO_THIRDS = math.sqrt(2.0 / 3.0)
+LOG_SIXTH = math.log(1.0 / 6.0)
+SPECK = 2.0**-60
 
 
 def half_of_features(matrix, u):
@@ -42,205 +46,232 @@ def half_of_features(matrix, u):
     return matrix[u * half : (u + 1) * half]
 
 
+def words_on_partitions(matrix):
+    return matrix.rearrange("(u p e) n -> p u (e n)", u=2, e=2)
+
+
 def tile_net_pa_kernel(tc, h1, coef2, sb2, sp2, b2, out):
     nc = tc.nc
     with (
         tc.tile_pool(name="keep", bufs=1) as keep,
-        tc.tile_pool(name="work", bufs=1) as work,
+        tc.tile_pool(name="waves", bufs=2) as waves,
+        tc.tile_pool(name="cubes", bufs=2) as cubes,
         tc.tile_pool(name="ring", bufs=2) as ring,
         tc.psum_pool(name="psum", bufs=2) as psum,
     ):
-        h1_rows = work.tile([P, ROW_TILES, FEATURES], BF16, tag="early")
-        h1_by_tile = h1.rearrange("(m p) i -> p m i", p=P)
-        for c in range(CHUNKS):
-            tiles = slice(c * TILES_PER_CHUNK, (c + 1) * TILES_PER_CHUNK)
-            nc.sync.dma_start(out=h1_rows[:, tiles, :], in_=h1_by_tile[:, tiles, :])
-        gain = keep.tile([P, PACK, OUTPUTS], BF16)
-        base_raw = keep.tile([P, PACK, OUTPUTS], BF16)
-        for u in range(2):
-            nc.sync.dma_start(
-                out=gain[:, 2 * u : 2 * u + 2, :],
-                in_=half_of_features(sp2, u).rearrange("(p e) o -> p e o", e=2),
-            )
-
-        def load_coef(piece):
-            coef_raw = ring.tile([P, PACK, O_PIECE * BASIS], BF16)
-            columns = slice(piece * O_PIECE, (piece + 1) * O_PIECE)
-            for u in range(2):
-                nc.sync.dma_start(
-                    out=coef_raw[:, 2 * u : 2 * u + 2, :],
-                    in_=half_of_features(coef2, u)[:, columns, :].rearrange("(p e) o g -> p e (o g)", e=2),
-                )
-            return coef_raw
-
-        coef_pieces = [load_coef(0), load_coef(1)]
-        for u in range(2):
-            nc.sync.dma_start(
-                out=base_raw[:, 2 * u : 2 * u + 2, :],
-                in_=half_of_features(sb2, u).rearrange("(p e) o -> p e o", e=2),
-            )
-        bias = keep.tile([P, OUTPUTS], BF16)
-        nc.sync.dma_start(out=bias[:], in_=b2.partition_broadcast(P))
-
-        identity = keep.tile([P, P], F32)
-        masks.make_identity(nc, identity[:])
-        h1_words = h1_rows[:].bitcast(F32)
         v = keep.tile([P, ALL], BF16, align_bytes=64)
-        v_words = v[:].bitcast(F32).rearrange("p (c m b u) -> p c m b u", c=CHUNKS, m=TILES_PER_CHUNK, u=2)
-        for c in range(CHUNKS):
-            turned = psum.tile([P, TILES_PER_CHUNK, 2, P], F32)
-            for m in range(TILES_PER_CHUNK):
-                for u in range(2):
-                    nc.tensor.transpose(
-                        out=turned[:, m, u, :],
-                        in_=h1_words[:, c * TILES_PER_CHUNK + m, u * P : (u + 1) * P],
-                        identity=identity[:],
-                    )
-            nc.scalar.copy(out=v_words[:, c], in_=turned[:].rearrange("p m u b -> p m b u"))
-
-        v_capped = work.tile([P, ALL], BF16, tag="early")
-        nc.vector.tensor_scalar_min(out=v_capped[:], in0=v[:], scalar1=V_CAP)
-        v_clipped = keep.tile([P, ALL], BF16)
-        nc.vector.tensor_scalar(
-            out=v_clipped[:], in0=v[:], scalar1=-V_EDGE, scalar2=V_EDGE, op0=ALU.max, op1=ALU.min
-        )
-        gate = work.tile([P, ALL], F32, tag="wide")
-        nc.scalar.activation(out=gate[:], in_=v_capped[:], func=ACT.Exp)
-        nc.scalar.activation(out=gate[:], in_=gate[:], func=ACT.Ln, bias=1.0)
-        nc.scalar.activation(out=gate[:], in_=gate[:], func=ACT.Tanh)
-
+        bias = keep.tile([P, OUTPUTS], BF16)
         w_codes = keep.tile([P, BRANCHES, OUTPUTS], U32, align_bytes=64)
         w_scales = keep.tile([P, BRANCHES, OUTPUTS], U8, align_bytes=64)
-        for piece in range(O_PIECES):
-            columns = slice(piece * O_PIECE, (piece + 1) * O_PIECE)
-            coef = coef_pieces[piece][:].rearrange("p t (o g) -> p t o g", g=BASIS)
-            w_grouped = work.tile([P, BASIS, O_PIECE, PACK], BF16, align_bytes=64)
-            for g0 in range(0, BASIS, G_RUN):
-                g_run = slice(g0, min(g0 + G_RUN, BASIS))
-                count = min(G_RUN, BASIS - g0)
-                nc.vector.tensor_tensor(
-                    out=w_grouped[:, g_run].rearrange("p g o t -> p o t g"),
-                    in0=coef[:, :, :, g_run].rearrange("p t o g -> p o t g"),
-                    in1=gain[:, :, columns]
-                    .rearrange("p t o -> p o t")
-                    .unsqueeze(3)
-                    .to_broadcast([P, O_PIECE, PACK, count]),
-                    op=ALU.mult,
-                )
-            if piece + 2 < O_PIECES:
-                coef_pieces.append(load_coef(piece + 2))
-            for g in range(BASIS):
-                nc.vector.quantize_mx(
-                    out=w_codes[:, g, columns].bitcast(FP8X4),
-                    scales=w_scales[:, g, columns],
-                    in_=w_grouped[:, g].rearrange("p o t -> p (o t)"),
-                )
-        base_grouped = work.tile([P, OUTPUTS, PACK], BF16, tag="slabs", align_bytes=64)
-        nc.vector.tensor_copy(out=base_grouped[:], in_=base_raw[:].rearrange("p t o -> p o t"))
-        nc.vector.quantize_mx(
-            out=w_codes[:, MISH, :].bitcast(FP8X4),
-            scales=w_scales[:, MISH, :],
-            in_=base_grouped[:].rearrange("p o t -> p (o t)"),
-        )
-
-        mish = work.tile([P, ALL], BF16, tag="slabs", align_bytes=64)
-        nc.vector.tensor_tensor(out=mish[:], in0=v[:], in1=gate[:], op=ALU.mult)
         mish_codes = keep.tile([P, ALL // PACK], U32, align_bytes=64)
         mish_scales = keep.tile([P, ALL // PACK], U8, align_bytes=64)
-        nc.vector.quantize_mx(out=mish_codes[:].bitcast(FP8X4), scales=mish_scales[:], in_=mish[:])
 
-        for c in range(CHUNKS):
-            vc = v_clipped[:, c * CHUNK : (c + 1) * CHUNK]
-            acc = [psum.tile([P, OUTPUTS], F32, name="acc", bufs=2 * TILES_PER_CHUNK) for m in range(TILES_PER_CHUNK)]
-
-            def multiply(codes, scales, branch, first, last):
-                for m in range(TILES_PER_CHUNK):
-                    rows = slice(m * P, (m + 1) * P)
-                    nc.tensor.matmul_mx(
-                        out=acc[m][:],
-                        lhsT=codes[:, rows].bitcast(FP8X4),
-                        lhsT_scale=scales[:, rows],
-                        rhs=w_codes[:, branch, :].bitcast(FP8X4),
-                        rhs_scale=w_scales[:, branch, :],
-                        start=first,
-                        stop=last,
-                    )
-
-            words = slice(c * CHUNK_WORDS, (c + 1) * CHUNK_WORDS)
-            multiply(mish_codes[:, words], mish_scales[:, words], MISH, True, False)
-
-            centred = work.tile([P, COMBS, CHUNK], F32, tag="wide")
-            for r in range(COMBS):
-                nc.scalar.activation(
-                    out=centred[:, r, :], in_=vc, func=ACT.Identity, scale=2.5 / 4.0, bias=(6.0 - r) / 4.0
-                )
-            window = work.tile([P, COMBS, CHUNK], BF16)
+        def fold_waves(c):
+            clipped = waves.tile([P, CHUNK], BF16)
             nc.vector.tensor_scalar(
-                out=window[:], in0=centred[:], scalar1=ROUND, scalar2=ROUND, op0=ALU.add, op1=ALU.subtract
+                out=clipped[:], in0=v[:, c * CHUNK : (c + 1) * CHUNK], scalar1=-V_EDGE, scalar2=V_EDGE,
+                op0=ALU.max, op1=ALU.min,
             )
+            below = waves.tile([P, CHUNK], F32)
+            nc.scalar.activation(out=below[:], in_=clipped[:], func=ACT.Identity, scale=2.5, bias=7.5)
+            from_centre = waves.tile([P, CHUNK], F32)
+            wave = waves.tile([P, 2, CHUNK], F32)
+            nc.scalar.activation(out=from_centre[:], in_=clipped[:], func=ACT.Abs, scale=2.5)
+            nc.scalar.activation(out=wave[:, 1, :], in_=clipped[:], func=ACT.Abs, scale=2.5, bias=-1.0)
+            nc.scalar.activation(out=wave[:, 0, :], in_=from_centre[:], func=ACT.Abs, bias=-6.0)
+            nc.scalar.activation(out=wave[:, 1, :], in_=wave[:, 1, :], func=ACT.Abs, bias=-4.0)
+            nc.scalar.activation(out=wave[:], in_=wave[:], func=ACT.Abs, bias=-2.0)
+            nc.vector.tensor_tensor(out=wave[:, 0, :], in0=from_centre[:], in1=wave[:, 0, :], op=ALU.min)
+            return below, wave
 
-            beta = work.tile([P, 2, CHUNK], F32)
-            from_centre = work.tile([P, CHUNK], F32)
-            folded_0 = work.tile([P, CHUNK], F32)
-            folded_1 = work.tile([P, CHUNK], F32)
-            nc.scalar.activation(out=from_centre[:], in_=vc, func=ACT.Abs, scale=2.5)
-            nc.scalar.activation(out=folded_1[:], in_=vc, func=ACT.Abs, scale=2.5, bias=-1.0)
-            nc.scalar.activation(out=folded_0[:], in_=from_centre[:], func=ACT.Abs, bias=-6.0)
-            nc.scalar.activation(out=folded_1[:], in_=folded_1[:], func=ACT.Abs, bias=-4.0)
-            nc.scalar.activation(out=folded_0[:], in_=folded_0[:], func=ACT.Abs, bias=-2.0)
-            nc.scalar.activation(out=folded_1[:], in_=folded_1[:], func=ACT.Abs, bias=-2.0)
-            nc.vector.tensor_tensor(out=beta[:, 0, :], in0=from_centre[:], in1=folded_0[:], op=ALU.min)
-            nc.scalar.activation(out=beta[:, 1, :], in_=folded_1[:], func=ACT.Identity, scale=-1.0, bias=2.0)
-
-            near = work.tile([P, 2, CHUNK], F32)
-            far = work.tile([P, 2, CHUNK], F32)
-            kink = work.tile([P, 2, CHUNK], F32)
+        def raise_to_cubes(wave):
+            kink = cubes.tile([P, 2, CHUNK], F32)
+            near = cubes.tile([P, 2, CHUNK], F32)
+            far = cubes.tile([P, 2, CHUNK], F32)
             nc.scalar.activation(
-                out=kink[:], in_=beta[:], func=ACT.Square, scale=ROOT_TWO_THIRDS, bias=-ROOT_TWO_THIRDS
+                out=kink[:], in_=wave[:], func=ACT.Square, scale=ROOT_TWO_THIRDS, bias=-ROOT_TWO_THIRDS
             )
-            nc.scalar.activation(out=near[:], in_=beta[:], func=ACT.Square, scale=ROOT_SIXTH)
-            nc.scalar.activation(out=far[:], in_=beta[:], func=ACT.Square, scale=-ROOT_SIXTH, bias=2.0 * ROOT_SIXTH)
-            nc.vector.scalar_tensor_tensor(
-                out=kink[:], in0=beta[:], scalar=1.0, in1=kink[:], op0=ALU.subtract, op1=ALU.mult
-            )
-            nc.vector.tensor_tensor(out=near[:], in0=beta[:], in1=near[:], op=ALU.mult)
-            nc.vector.scalar_tensor_tensor(
-                out=far[:], in0=beta[:], scalar=2.0, in1=far[:], op0=ALU.subtract, op1=ALU.mult
-            )
-            periodic = work.tile([P, COMBS, CHUNK], BF16)
-            nc.vector.scalar_tensor_tensor(
-                out=periodic[:, 0:2, :], in0=kink[:], scalar=0.0, in1=near[:], op0=ALU.max, op1=ALU.subtract
-            )
-            nc.vector.scalar_tensor_tensor(
-                out=periodic[:, 2:4, :], in0=kink[:], scalar=0.0, in1=far[:], op0=ALU.min, op1=ALU.subtract
-            )
+            nc.scalar.activation(out=far[:, 1, :], in_=wave[:, 1, :], func=ACT.Abs, scale=-1.0, bias=2.0)
+            nc.scalar.activation(out=near[:], in_=wave[:], func=ACT.Ln, bias=SPECK)
+            nc.scalar.activation(out=far[:, 0, :], in_=wave[:, 0, :], func=ACT.Ln, scale=-1.0, bias=2.0)
+            nc.scalar.activation(out=far[:, 1, :], in_=far[:, 1, :], func=ACT.Ln, bias=SPECK)
+            nc.scalar.activation(out=near[:], in_=near[:], func=ACT.Exp, scale=3.0, bias=LOG_SIXTH)
+            nc.scalar.activation(out=far[:], in_=far[:], func=ACT.Exp, scale=3.0, bias=LOG_SIXTH)
+            return kink, near, far
 
-            for r in range(COMBS):
-                members = list(range(r, BASIS, COMBS))
-                sign = -1.0 if r < 2 else 1.0
-                inside = work.tile([P, COMBS, CHUNK], BF16)
-                for n in range(len(members)):
-                    nc.vector.tensor_scalar(
-                        out=inside[:, n, :], in0=window[:, r, :], scalar1=float(n), scalar2=sign,
-                        op0=ALU.is_equal, op1=ALU.mult,
+        with (
+            tc.tile_pool(name="early", bufs=1) as early,
+            tc.tile_pool(name="stream", bufs=2) as stream,
+        ):
+            h1_rows = early.tile([P, ROW_TILES, FEATURES], BF16, tag="h1")
+            h1_by_tile = h1.rearrange("(m p) i -> p m i", p=P)
+
+            def load_h1(c):
+                tiles = slice(c * TILES_PER_CHUNK, (c + 1) * TILES_PER_CHUNK)
+                nc.sync.dma_start(out=h1_rows[:, tiles, :], in_=h1_by_tile[:, tiles, :])
+
+            def load_coef(piece):
+                coef_raw = stream.tile([P, PACK, O_PIECE * BASIS], BF16)
+                columns = slice(piece * O_PIECE, (piece + 1) * O_PIECE)
+                for u in range(2):
+                    nc.sync.dma_start(
+                        out=coef_raw[:, 2 * u : 2 * u + 2, :],
+                        in_=half_of_features(coef2, u)[:, columns, :].rearrange("(p e) o g -> p e (o g)", e=2),
                     )
-                slabs = work.tile([P, COMBS, CHUNK], BF16, tag="slabs", align_bytes=64)
-                nc.vector.tensor_tensor(
-                    out=slabs[:, 0 : len(members), :],
-                    in0=periodic[:, r : r + 1, :].to_broadcast([P, len(members), CHUNK]),
-                    in1=inside[:, 0 : len(members), :],
-                    op=ALU.mult,
-                )
-                codes = ring.tile([P, COMBS, CHUNK_WORDS], U32, align_bytes=64, bufs=3)
-                scales = ring.tile([P, COMBS, CHUNK_WORDS], U8, align_bytes=64, bufs=3)
-                for n, g in enumerate(members):
+                return coef_raw
+
+            gain = early.tile([P, PACK, OUTPUTS], BF16)
+            nc.sync.dma_start(out=gain[:].rearrange("p (u e) o -> p u (e o)", u=2), in_=words_on_partitions(sp2))
+            coef_pieces = [load_coef(0)]
+            for c in range(CHUNKS):
+                load_h1(c)
+            coef_pieces.append(load_coef(1))
+            base_raw = early.tile([P, PACK, OUTPUTS], BF16)
+            nc.sync.dma_start(
+                out=base_raw[:].rearrange("p (u e) o -> p u (e o)", u=2), in_=words_on_partitions(sb2)
+            )
+            nc.sync.dma_start(out=bias[:], in_=b2.partition_broadcast(P))
+
+            identity = early.tile([P, P], F32)
+            masks.make_identity(nc, identity[:])
+            h1_words = h1_rows[:].bitcast(F32)
+            v_words = v[:].bitcast(F32).rearrange("p (c m b u) -> p c m b u", c=CHUNKS, m=TILES_PER_CHUNK, u=2)
+            for c in range(CHUNKS):
+                turned = psum.tile([P, TILES_PER_CHUNK, 2, P], F32)
+                for m in range(TILES_PER_CHUNK):
+                    for u in range(2):
+                        nc.tensor.transpose(
+                            out=turned[:, m, u, :],
+                            in_=h1_words[:, c * TILES_PER_CHUNK + m, u * P : (u + 1) * P],
+                            identity=identity[:],
+                        )
+                nc.scalar.copy(out=v_words[:, c], in_=turned[:].rearrange("p m u b -> p m b u"))
+
+            below, wave = fold_waves(0)
+            kink, near, far = raise_to_cubes(wave)
+
+            v_capped = early.tile([P, ALL], BF16, tag="h1")
+            nc.vector.tensor_scalar_min(out=v_capped[:], in0=v[:], scalar1=V_CAP)
+            gate = early.tile([P, ALL], F32)
+            nc.scalar.activation(out=gate[:], in_=v_capped[:], func=ACT.Exp)
+            nc.scalar.activation(out=gate[:], in_=gate[:], func=ACT.Ln, bias=1.0)
+            nc.scalar.activation(out=gate[:], in_=gate[:], func=ACT.Tanh)
+
+            for piece in range(O_PIECES):
+                columns = slice(piece * O_PIECE, (piece + 1) * O_PIECE)
+                coef = coef_pieces[piece][:].rearrange("p t (o g) -> p t o g", g=BASIS)
+                w_grouped = early.tile([P, BASIS, O_PIECE, PACK], BF16, align_bytes=64)
+                for g0 in range(0, BASIS, G_RUN):
+                    g_run = slice(g0, min(g0 + G_RUN, BASIS))
+                    count = min(G_RUN, BASIS - g0)
+                    nc.vector.tensor_tensor(
+                        out=w_grouped[:, g_run].rearrange("p g o t -> p o t g"),
+                        in0=coef[:, :, :, g_run].rearrange("p t o g -> p o t g"),
+                        in1=gain[:, :, columns]
+                        .rearrange("p t o -> p o t")
+                        .unsqueeze(3)
+                        .to_broadcast([P, O_PIECE, PACK, count]),
+                        op=ALU.mult,
+                    )
+                if piece + 2 < O_PIECES:
+                    coef_pieces.append(load_coef(piece + 2))
+                for g in range(BASIS):
                     nc.vector.quantize_mx(
-                        out=codes[:, n, :].bitcast(FP8X4), scales=scales[:, n, :], in_=slabs[:, n, :]
+                        out=w_codes[:, g, columns].bitcast(FP8X4),
+                        scales=w_scales[:, g, columns],
+                        in_=w_grouped[:, g].rearrange("p o t -> p (o t)"),
                     )
-                    multiply(codes[:, n, :], scales[:, n, :], g, False, r == COMBS - 1 and g == members[-1])
+            base_grouped = early.tile([P, OUTPUTS, PACK], BF16, tag="mish", align_bytes=64)
+            nc.scalar.copy(out=base_grouped[:], in_=base_raw[:].rearrange("p t o -> p o t"))
+            nc.vector.quantize_mx(
+                out=w_codes[:, MISH, :].bitcast(FP8X4),
+                scales=w_scales[:, MISH, :],
+                in_=base_grouped[:].rearrange("p o t -> p (o t)"),
+            )
 
+            mish = early.tile([P, ALL], BF16, tag="mish", align_bytes=64)
+            nc.vector.tensor_tensor(out=mish[:], in0=v[:], in1=gate[:], op=ALU.mult)
+            nc.vector.quantize_mx(out=mish_codes[:].bitcast(FP8X4), scales=mish_scales[:], in_=mish[:])
+
+        def store(c, acc):
             for m in range(TILES_PER_CHUNK):
                 result = ring.tile([P, OUTPUTS], F32)
                 nc.vector.tensor_tensor(out=result[:], in0=acc[m][:], in1=bias[:], op=ALU.add)
                 row0 = (c * TILES_PER_CHUNK + m) * P
                 nc.sync.dma_start(out=out[row0 : row0 + P, :], in_=result[:])
+
+        with tc.tile_pool(name="basis", bufs=1) as basis:
+            for c in range(CHUNKS):
+                cell = basis.tile([P, CHUNK], BF16)
+                nc.vector.tensor_scalar(
+                    out=cell[:], in0=below[:], scalar1=ROUND, scalar2=ROUND, op0=ALU.add, op1=ALU.subtract
+                )
+                quarter = basis.tile([P, COMBS, CHUNK], BF16)
+                for row, r in enumerate(COMB_OF_ROW):
+                    nc.vector.tensor_scalar(
+                        out=quarter[:, row, :], in0=cell[:], scalar1=0.25, scalar2=-(r + 1.5) / 4.0,
+                        op0=ALU.mult, op1=ALU.add,
+                    )
+
+                nc.vector.scalar_tensor_tensor(
+                    out=kink[:], in0=wave[:], scalar=1.0, in1=kink[:], op0=ALU.subtract, op1=ALU.mult
+                )
+                periodic = basis.tile([P, COMBS, CHUNK], BF16)
+                nc.vector.scalar_tensor_tensor(
+                    out=periodic[:, 0:2, :], in0=kink[:], scalar=0.0, in1=near[:], op0=ALU.max, op1=ALU.subtract,
+                    reverse1=True,
+                )
+                nc.vector.scalar_tensor_tensor(
+                    out=periodic[:, 2:4, :], in0=kink[:], scalar=0.0, in1=far[:], op0=ALU.min, op1=ALU.add
+                )
+
+                if c + 1 < CHUNKS:
+                    below, wave = fold_waves(c + 1)
+                    kink, near, far = raise_to_cubes(wave)
+
+                if c > 0:
+                    store(c - 1, acc)
+                acc = [
+                    psum.tile([P, OUTPUTS], F32, name="acc", bufs=2 * TILES_PER_CHUNK)
+                    for m in range(TILES_PER_CHUNK)
+                ]
+
+                def multiply(codes, scales, branch, first, last):
+                    for m in range(TILES_PER_CHUNK):
+                        rows = slice(m * P, (m + 1) * P)
+                        nc.tensor.matmul_mx(
+                            out=acc[m][:],
+                            lhsT=codes[:, rows].bitcast(FP8X4),
+                            lhsT_scale=scales[:, rows],
+                            rhs=w_codes[:, branch, :].bitcast(FP8X4),
+                            rhs_scale=w_scales[:, branch, :],
+                            start=first,
+                            stop=last,
+                        )
+
+                words = slice(c * CHUNK_WORDS, (c + 1) * CHUNK_WORDS)
+                multiply(mish_codes[:, words], mish_scales[:, words], MISH, True, False)
+
+                for n in range(WINDOWS):
+                    rows_used = [row for row in range(COMBS) if COMB_OF_ROW[row] + COMBS * n < BASIS]
+                    count = len(rows_used)
+                    inside = basis.tile([P, COMBS, CHUNK], BF16, bufs=2)
+                    nc.vector.tensor_scalar(
+                        out=inside[:, 0:count, :], in0=quarter[:, 0:count, :], scalar1=ROUND, scalar2=ROUND + n,
+                        op0=ALU.add, op1=ALU.is_equal,
+                    )
+                    slabs = basis.tile([P, COMBS, CHUNK], BF16, align_bytes=64, bufs=2)
+                    nc.vector.tensor_tensor(
+                        out=slabs[:, 0:count, :], in0=periodic[:, 0:count, :], in1=inside[:, 0:count, :], op=ALU.mult
+                    )
+                    codes = ring.tile([P, COMBS, CHUNK_WORDS], U32, align_bytes=64, bufs=3)
+                    scales = ring.tile([P, COMBS, CHUNK_WORDS], U8, align_bytes=64, bufs=3)
+                    nc.vector.quantize_mx(
+                        out=codes[:, 0:count, :].rearrange("p r w -> p (r w)").bitcast(FP8X4),
+                        scales=scales[:, 0:count, :].rearrange("p r w -> p (r w)"),
+                        in_=slabs[:, 0:count, :].rearrange("p r k -> p (r k)"),
+                    )
+                    for row in rows_used:
+                        g = COMB_OF_ROW[row] + COMBS * n
+                        multiply(codes[:, row, :], scales[:, row, :], g, False, g == BASIS - 1)
+            store(CHUNKS - 1, acc)

@@ -32,6 +32,7 @@ ALL = CHUNKS * CHUNK
 O_PIECE = 128
 O_PIECES = OUTPUTS // O_PIECE
 G_RUN = 4
+GPSIMD_RUN = 2
 
 ROUND = 12582912.0
 V_EDGE = 3.25
@@ -147,6 +148,22 @@ def tile_net_pa_kernel(tc, h1, coef2, sb2, sp2, b2, out):
                         )
                 nc.scalar.copy(out=v_words[:, c], in_=turned[:].rearrange("p m u b -> p m b u"))
 
+            identity_bf = early.tile([P, P], BF16)
+            masks.make_identity(nc, identity_bf[:])
+            gain_banks = []
+            for pair in range(O_PIECES // 2):
+                gain_bank = psum.tile([P, 2, PACK, O_PIECE], BF16)
+                for half in range(2):
+                    piece = 2 * pair + half
+                    nc.tensor.matmul(
+                        out=gain_bank[:, half],
+                        lhsT=identity_bf[:],
+                        rhs=gain[:, :, piece * O_PIECE : (piece + 1) * O_PIECE],
+                        start=True,
+                        stop=True,
+                    )
+                gain_banks.append(gain_bank)
+
             below, wave = fold_waves(0)
             kink, near, far = raise_to_cubes(wave)
 
@@ -164,13 +181,14 @@ def tile_net_pa_kernel(tc, h1, coef2, sb2, sp2, b2, out):
                 for g0 in range(0, BASIS, G_RUN):
                     g_run = slice(g0, min(g0 + G_RUN, BASIS))
                     count = min(G_RUN, BASIS - g0)
-                    nc.vector.tensor_tensor(
+                    if g0 == GPSIMD_RUN * G_RUN:
+                        engine, factor = nc.gpsimd, gain[:, :, columns]
+                    else:
+                        engine, factor = nc.vector, gain_banks[piece // 2][:, piece % 2]
+                    engine.tensor_tensor(
                         out=w_grouped[:, g_run].rearrange("p g o t -> p o t g"),
                         in0=coef[:, :, :, g_run].rearrange("p t o g -> p o t g"),
-                        in1=gain[:, :, columns]
-                        .rearrange("p t o -> p o t")
-                        .unsqueeze(3)
-                        .to_broadcast([P, O_PIECE, PACK, count]),
+                        in1=factor.rearrange("p t o -> p o t").unsqueeze(3).to_broadcast([P, O_PIECE, PACK, count]),
                         op=ALU.mult,
                     )
                 if piece + 2 < O_PIECES:

@@ -32,7 +32,7 @@ ALL = CHUNKS * CHUNK
 O_PIECE = 128
 O_PIECES = OUTPUTS // O_PIECE
 G_RUN = 4
-GPSIMD_RUN = 2
+GPSIMD_FIRST_G = 10
 
 ROUND = 12582912.0
 V_EDGE = 3.25
@@ -121,10 +121,11 @@ def tile_net_pa_kernel(tc, h1, coef2, sb2, sp2, b2, out):
                     )
                 return coef_raw
 
+            load_h1(0)
             gain = early.tile([P, PACK, OUTPUTS], BF16)
             nc.sync.dma_start(out=gain[:].rearrange("p (u e) o -> p u (e o)", u=2), in_=words_on_partitions(sp2))
             coef_pieces = [load_coef(0)]
-            for c in range(CHUNKS):
+            for c in range(1, CHUNKS):
                 load_h1(c)
             coef_pieces.append(load_coef(1))
             base_raw = early.tile([P, PACK, OUTPUTS], BF16)
@@ -132,21 +133,6 @@ def tile_net_pa_kernel(tc, h1, coef2, sb2, sp2, b2, out):
                 out=base_raw[:].rearrange("p (u e) o -> p u (e o)", u=2), in_=words_on_partitions(sb2)
             )
             nc.sync.dma_start(out=bias[:], in_=b2.partition_broadcast(P))
-
-            identity = early.tile([P, P], F32)
-            masks.make_identity(nc, identity[:])
-            h1_words = h1_rows[:].bitcast(F32)
-            v_words = v[:].bitcast(F32).rearrange("p (c m b u) -> p c m b u", c=CHUNKS, m=TILES_PER_CHUNK, u=2)
-            for c in range(CHUNKS):
-                turned = psum.tile([P, TILES_PER_CHUNK, 2, P], F32)
-                for m in range(TILES_PER_CHUNK):
-                    for u in range(2):
-                        nc.tensor.transpose(
-                            out=turned[:, m, u, :],
-                            in_=h1_words[:, c * TILES_PER_CHUNK + m, u * P : (u + 1) * P],
-                            identity=identity[:],
-                        )
-                nc.scalar.copy(out=v_words[:, c], in_=turned[:].rearrange("p m u b -> p m b u"))
 
             identity_bf = early.tile([P, P], BF16)
             masks.make_identity(nc, identity_bf[:])
@@ -164,6 +150,21 @@ def tile_net_pa_kernel(tc, h1, coef2, sb2, sp2, b2, out):
                     )
                 gain_banks.append(gain_bank)
 
+            identity = early.tile([P, P], F32)
+            masks.make_identity(nc, identity[:])
+            h1_words = h1_rows[:].bitcast(F32)
+            v_words = v[:].bitcast(F32).rearrange("p (c m b u) -> p c m b u", c=CHUNKS, m=TILES_PER_CHUNK, u=2)
+            for c in range(CHUNKS):
+                turned = psum.tile([P, TILES_PER_CHUNK, 2, P], F32)
+                for m in range(TILES_PER_CHUNK):
+                    for u in range(2):
+                        nc.tensor.transpose(
+                            out=turned[:, m, u, :],
+                            in_=h1_words[:, c * TILES_PER_CHUNK + m, u * P : (u + 1) * P],
+                            identity=identity[:],
+                        )
+                nc.scalar.copy(out=v_words[:, c], in_=turned[:].rearrange("p m u b -> p m b u"))
+
             below, wave = fold_waves(0)
             kink, near, far = raise_to_cubes(wave)
 
@@ -178,18 +179,22 @@ def tile_net_pa_kernel(tc, h1, coef2, sb2, sp2, b2, out):
                 columns = slice(piece * O_PIECE, (piece + 1) * O_PIECE)
                 coef = coef_pieces[piece][:].rearrange("p t (o g) -> p t o g", g=BASIS)
                 w_grouped = early.tile([P, BASIS, O_PIECE, PACK], BF16, align_bytes=64)
-                for g0 in range(0, BASIS, G_RUN):
-                    g_run = slice(g0, min(g0 + G_RUN, BASIS))
-                    count = min(G_RUN, BASIS - g0)
-                    if g0 == GPSIMD_RUN * G_RUN:
-                        engine, factor = nc.gpsimd, gain[:, :, columns]
-                    else:
-                        engine, factor = nc.vector, gain_banks[piece // 2][:, piece % 2]
+
+                def scale_run(engine, factor, first, last):
+                    g_run = slice(first, last)
                     engine.tensor_tensor(
                         out=w_grouped[:, g_run].rearrange("p g o t -> p o t g"),
                         in0=coef[:, :, :, g_run].rearrange("p t o g -> p o t g"),
-                        in1=factor.rearrange("p t o -> p o t").unsqueeze(3).to_broadcast([P, O_PIECE, PACK, count]),
+                        in1=factor.rearrange("p t o -> p o t")
+                        .unsqueeze(3)
+                        .to_broadcast([P, O_PIECE, PACK, last - first]),
                         op=ALU.mult,
+                    )
+
+                scale_run(nc.gpsimd, gain[:, :, columns], GPSIMD_FIRST_G, BASIS)
+                for first in range(0, GPSIMD_FIRST_G, G_RUN):
+                    scale_run(
+                        nc.vector, gain_banks[piece // 2][:, piece % 2], first, min(first + G_RUN, GPSIMD_FIRST_G)
                     )
                 if piece + 2 < O_PIECES:
                     coef_pieces.append(load_coef(piece + 2))

@@ -31,8 +31,8 @@ ALL = CHUNKS * CHUNK
 
 O_PIECE = 128
 O_PIECES = OUTPUTS // O_PIECE
-G_RUN = 4
-GPSIMD_FIRST_G = 10
+GPSIMD_FIRST_G = 11
+G_PAIR = 2
 
 ROUND = 12582912.0
 V_EDGE = 3.25
@@ -134,21 +134,10 @@ def tile_net_pa_kernel(tc, h1, coef2, sb2, sp2, b2, out):
             )
             nc.sync.dma_start(out=bias[:], in_=b2.partition_broadcast(P))
 
+            gain_grouped = early.tile([P, OUTPUTS, PACK], BF16)
+            nc.vector.tensor_copy(out=gain_grouped[:], in_=gain[:].rearrange("p t o -> p o t"))
             identity_bf = early.tile([P, P], BF16)
             masks.make_identity(nc, identity_bf[:])
-            gain_banks = []
-            for pair in range(O_PIECES // 2):
-                gain_bank = psum.tile([P, 2, PACK, O_PIECE], BF16)
-                for half in range(2):
-                    piece = 2 * pair + half
-                    nc.tensor.matmul(
-                        out=gain_bank[:, half],
-                        lhsT=identity_bf[:],
-                        rhs=gain[:, :, piece * O_PIECE : (piece + 1) * O_PIECE],
-                        start=True,
-                        stop=True,
-                    )
-                gain_banks.append(gain_bank)
 
             identity = early.tile([P, P], F32)
             masks.make_identity(nc, identity[:])
@@ -177,24 +166,33 @@ def tile_net_pa_kernel(tc, h1, coef2, sb2, sp2, b2, out):
 
             for piece in range(O_PIECES):
                 columns = slice(piece * O_PIECE, (piece + 1) * O_PIECE)
-                coef = coef_pieces[piece][:].rearrange("p t (o g) -> p t o g", g=BASIS)
-                w_grouped = early.tile([P, BASIS, O_PIECE, PACK], BF16, align_bytes=64)
+                coef = coef_pieces[piece][:].rearrange("p t (o g) -> p g o t", g=BASIS)
+                piece_gain = gain_grouped[:, columns].rearrange("p o t -> p (o t)")
+                w_grouped = early.tile([P, BASIS, O_PIECE * PACK], BF16, align_bytes=64)
 
-                def scale_run(engine, factor, first, last):
-                    g_run = slice(first, last)
-                    engine.tensor_tensor(
-                        out=w_grouped[:, g_run].rearrange("p g o t -> p o t g"),
-                        in0=coef[:, :, :, g_run].rearrange("p t o g -> p o t g"),
-                        in1=factor.rearrange("p t o -> p o t")
-                        .unsqueeze(3)
-                        .to_broadcast([P, O_PIECE, PACK, last - first]),
+                for g in range(GPSIMD_FIRST_G, BASIS):
+                    nc.gpsimd.tensor_tensor(
+                        out=w_grouped[:, g].rearrange("p (o t) -> p o t", t=PACK),
+                        in0=coef[:, g],
+                        in1=gain_grouped[:, columns],
                         op=ALU.mult,
                     )
-
-                scale_run(nc.gpsimd, gain[:, :, columns], GPSIMD_FIRST_G, BASIS)
-                for first in range(0, GPSIMD_FIRST_G, G_RUN):
-                    scale_run(
-                        nc.vector, gain_banks[piece // 2][:, piece % 2], first, min(first + G_RUN, GPSIMD_FIRST_G)
+                for first in range(0, GPSIMD_FIRST_G, G_PAIR):
+                    g_run = range(first, min(first + G_PAIR, GPSIMD_FIRST_G))
+                    bank = psum.tile([P, G_PAIR, O_PIECE * PACK], BF16)
+                    for k, g in enumerate(g_run):
+                        nc.tensor.matmul(
+                            out=bank[:, k].rearrange("p (o t) -> p o t", t=PACK),
+                            lhsT=identity_bf[:],
+                            rhs=coef[:, g],
+                            start=True,
+                            stop=True,
+                        )
+                    nc.vector.tensor_tensor(
+                        out=w_grouped[:, first : first + len(g_run)],
+                        in0=bank[:, 0 : len(g_run)],
+                        in1=piece_gain.unsqueeze(1).to_broadcast([P, len(g_run), O_PIECE * PACK]),
+                        op=ALU.mult,
                     )
                 if piece + 2 < O_PIECES:
                     coef_pieces.append(load_coef(piece + 2))
@@ -202,7 +200,7 @@ def tile_net_pa_kernel(tc, h1, coef2, sb2, sp2, b2, out):
                     nc.vector.quantize_mx(
                         out=w_codes[:, g, columns].bitcast(FP8X4),
                         scales=w_scales[:, g, columns],
-                        in_=w_grouped[:, g].rearrange("p o t -> p (o t)"),
+                        in_=w_grouped[:, g],
                     )
             base_grouped = early.tile([P, OUTPUTS, PACK], BF16, tag="mish", align_bytes=64)
             nc.scalar.copy(out=base_grouped[:], in_=base_raw[:].rearrange("p t o -> p o t"))

@@ -32,7 +32,7 @@ ALL = CHUNKS * CHUNK
 O_PIECE = 128
 O_PIECES = OUTPUTS // O_PIECE
 GPSIMD_FIRST_G = 11
-G_PAIR = 2
+O_BLOCK = 16
 
 ROUND = 12582912.0
 V_EDGE = 3.25
@@ -57,6 +57,7 @@ def tile_net_pa_kernel(tc, h1, coef2, sb2, sp2, b2, out):
         tc.tile_pool(name="keep", bufs=1) as keep,
         tc.tile_pool(name="waves", bufs=2) as waves,
         tc.tile_pool(name="cubes", bufs=2) as cubes,
+        tc.tile_pool(name="gates", bufs=2) as gates,
         tc.tile_pool(name="ring", bufs=2) as ring,
         tc.psum_pool(name="psum", bufs=2) as psum,
     ):
@@ -64,15 +65,20 @@ def tile_net_pa_kernel(tc, h1, coef2, sb2, sp2, b2, out):
         bias = keep.tile([P, OUTPUTS], BF16)
         w_codes = keep.tile([P, BRANCHES, OUTPUTS], U32, align_bytes=64)
         w_scales = keep.tile([P, BRANCHES, OUTPUTS], U8, align_bytes=64)
-        mish_codes = keep.tile([P, ALL // PACK], U32, align_bytes=64)
-        mish_scales = keep.tile([P, ALL // PACK], U8, align_bytes=64)
+        base_raw = keep.tile([P, PACK, OUTPUTS], BF16)
+        base_grouped = keep.tile([P, OUTPUTS, PACK], BF16, align_bytes=64)
 
-        def fold_waves(c):
+        def clip(c):
+            v_chunk = v[:, c * CHUNK : (c + 1) * CHUNK]
             clipped = waves.tile([P, CHUNK], BF16)
             nc.vector.tensor_scalar(
-                out=clipped[:], in0=v[:, c * CHUNK : (c + 1) * CHUNK], scalar1=-V_EDGE, scalar2=V_EDGE,
-                op0=ALU.max, op1=ALU.min,
+                out=clipped[:], in0=v_chunk, scalar1=-V_EDGE, scalar2=V_EDGE, op0=ALU.max, op1=ALU.min
             )
+            capped = gates.tile([P, CHUNK], BF16)
+            nc.vector.tensor_scalar_min(out=capped[:], in0=v_chunk, scalar1=V_CAP)
+            return clipped, capped
+
+        def fold_waves(clipped, capped):
             below = waves.tile([P, CHUNK], F32)
             nc.scalar.activation(out=below[:], in_=clipped[:], func=ACT.Identity, scale=2.5, bias=7.5)
             from_centre = waves.tile([P, CHUNK], F32)
@@ -82,10 +88,14 @@ def tile_net_pa_kernel(tc, h1, coef2, sb2, sp2, b2, out):
             nc.scalar.activation(out=wave[:, 0, :], in_=from_centre[:], func=ACT.Abs, bias=-6.0)
             nc.scalar.activation(out=wave[:, 1, :], in_=wave[:, 1, :], func=ACT.Abs, bias=-4.0)
             nc.scalar.activation(out=wave[:], in_=wave[:], func=ACT.Abs, bias=-2.0)
-            nc.vector.tensor_tensor(out=wave[:, 0, :], in0=from_centre[:], in1=wave[:, 0, :], op=ALU.min)
-            return below, wave
+            gate = gates.tile([P, CHUNK], F32)
+            nc.scalar.activation(out=gate[:], in_=capped[:], func=ACT.Exp)
+            return below, from_centre, wave, gate
 
-        def raise_to_cubes(wave):
+        def finish_wave(from_centre, wave):
+            nc.vector.tensor_tensor(out=wave[:, 0, :], in0=from_centre[:], in1=wave[:, 0, :], op=ALU.min)
+
+        def raise_to_cubes(wave, gate):
             kink = cubes.tile([P, 2, CHUNK], F32)
             near = cubes.tile([P, 2, CHUNK], F32)
             far = cubes.tile([P, 2, CHUNK], F32)
@@ -96,8 +106,10 @@ def tile_net_pa_kernel(tc, h1, coef2, sb2, sp2, b2, out):
             nc.scalar.activation(out=near[:], in_=wave[:], func=ACT.Ln, bias=SPECK)
             nc.scalar.activation(out=far[:, 0, :], in_=wave[:, 0, :], func=ACT.Ln, scale=-1.0, bias=2.0)
             nc.scalar.activation(out=far[:, 1, :], in_=far[:, 1, :], func=ACT.Ln, bias=SPECK)
+            nc.scalar.activation(out=gate[:], in_=gate[:], func=ACT.Ln, bias=1.0)
             nc.scalar.activation(out=near[:], in_=near[:], func=ACT.Exp, scale=3.0, bias=LOG_SIXTH)
             nc.scalar.activation(out=far[:], in_=far[:], func=ACT.Exp, scale=3.0, bias=LOG_SIXTH)
+            nc.scalar.activation(out=gate[:], in_=gate[:], func=ACT.Tanh)
             return kink, near, far
 
         with (
@@ -128,7 +140,6 @@ def tile_net_pa_kernel(tc, h1, coef2, sb2, sp2, b2, out):
             for c in range(1, CHUNKS):
                 load_h1(c)
             coef_pieces.append(load_coef(1))
-            base_raw = early.tile([P, PACK, OUTPUTS], BF16)
             nc.sync.dma_start(
                 out=base_raw[:].rearrange("p (u e) o -> p u (e o)", u=2), in_=words_on_partitions(sb2)
             )
@@ -144,7 +155,7 @@ def tile_net_pa_kernel(tc, h1, coef2, sb2, sp2, b2, out):
             h1_words = h1_rows[:].bitcast(F32)
             v_words = v[:].bitcast(F32).rearrange("p (c m b u) -> p c m b u", c=CHUNKS, m=TILES_PER_CHUNK, u=2)
             for c in range(CHUNKS):
-                turned = psum.tile([P, TILES_PER_CHUNK, 2, P], F32)
+                turned = psum.tile([P, TILES_PER_CHUNK, 2, P], F32, tag="turn", bufs=4)
                 for m in range(TILES_PER_CHUNK):
                     for u in range(2):
                         nc.tensor.transpose(
@@ -154,44 +165,40 @@ def tile_net_pa_kernel(tc, h1, coef2, sb2, sp2, b2, out):
                         )
                 nc.scalar.copy(out=v_words[:, c], in_=turned[:].rearrange("p m u b -> p m b u"))
 
-            below, wave = fold_waves(0)
-            kink, near, far = raise_to_cubes(wave)
-
-            v_capped = early.tile([P, ALL], BF16, tag="h1")
-            nc.vector.tensor_scalar_min(out=v_capped[:], in0=v[:], scalar1=V_CAP)
-            gate = early.tile([P, ALL], F32)
-            nc.scalar.activation(out=gate[:], in_=v_capped[:], func=ACT.Exp)
-            nc.scalar.activation(out=gate[:], in_=gate[:], func=ACT.Ln, bias=1.0)
-            nc.scalar.activation(out=gate[:], in_=gate[:], func=ACT.Tanh)
+            clipped, capped = clip(0)
+            below, from_centre, wave, gate = fold_waves(clipped, capped)
 
             for piece in range(O_PIECES):
                 columns = slice(piece * O_PIECE, (piece + 1) * O_PIECE)
-                coef = coef_pieces[piece][:].rearrange("p t (o g) -> p g o t", g=BASIS)
-                piece_gain = gain_grouped[:, columns].rearrange("p o t -> p (o t)")
-                w_grouped = early.tile([P, BASIS, O_PIECE * PACK], BF16, align_bytes=64)
+                coef = coef_pieces[piece][:].rearrange("p t (o g) -> p t o g", g=BASIS)
+                w_grouped = early.tile([P, BASIS, O_PIECE, PACK], BF16, align_bytes=64)
 
                 for g in range(GPSIMD_FIRST_G, BASIS):
                     nc.gpsimd.tensor_tensor(
-                        out=w_grouped[:, g].rearrange("p (o t) -> p o t", t=PACK),
-                        in0=coef[:, g],
+                        out=w_grouped[:, g],
+                        in0=coef[:, :, :, g].rearrange("p t o -> p o t"),
                         in1=gain_grouped[:, columns],
                         op=ALU.mult,
                     )
-                for first in range(0, GPSIMD_FIRST_G, G_PAIR):
-                    g_run = range(first, min(first + G_PAIR, GPSIMD_FIRST_G))
-                    bank = psum.tile([P, G_PAIR, O_PIECE * PACK], BF16)
-                    for k, g in enumerate(g_run):
+                for o in range(0, O_PIECE, O_BLOCK):
+                    bank = psum.tile([P, GPSIMD_FIRST_G, O_BLOCK, PACK], BF16, tag="turn", bufs=4)
+                    for u in range(2):
                         nc.tensor.matmul(
-                            out=bank[:, k].rearrange("p (o t) -> p o t", t=PACK),
+                            out=bank[:, :, :, 2 * u : 2 * u + 2].rearrange("p g o e -> p o g e"),
                             lhsT=identity_bf[:],
-                            rhs=coef[:, g],
+                            rhs=coef[:, 2 * u : 2 * u + 2, o : o + O_BLOCK, 0:GPSIMD_FIRST_G].rearrange(
+                                "p e o g -> p o g e"
+                            ),
                             start=True,
                             stop=True,
                         )
+                    block_gain = gain_grouped[:, piece * O_PIECE + o : piece * O_PIECE + o + O_BLOCK]
                     nc.vector.tensor_tensor(
-                        out=w_grouped[:, first : first + len(g_run)],
-                        in0=bank[:, 0 : len(g_run)],
-                        in1=piece_gain.unsqueeze(1).to_broadcast([P, len(g_run), O_PIECE * PACK]),
+                        out=w_grouped[:, 0:GPSIMD_FIRST_G, o : o + O_BLOCK].rearrange("p g o t -> p g (o t)"),
+                        in0=bank[:].rearrange("p g o t -> p g (o t)"),
+                        in1=block_gain.rearrange("p o t -> p (o t)")
+                        .unsqueeze(1)
+                        .to_broadcast([P, GPSIMD_FIRST_G, O_BLOCK * PACK]),
                         op=ALU.mult,
                     )
                 if piece + 2 < O_PIECES:
@@ -200,19 +207,12 @@ def tile_net_pa_kernel(tc, h1, coef2, sb2, sp2, b2, out):
                     nc.vector.quantize_mx(
                         out=w_codes[:, g, columns].bitcast(FP8X4),
                         scales=w_scales[:, g, columns],
-                        in_=w_grouped[:, g],
+                        in_=w_grouped[:, g].rearrange("p o t -> p (o t)"),
                     )
-            base_grouped = early.tile([P, OUTPUTS, PACK], BF16, tag="mish", align_bytes=64)
+                if piece == 0:
+                    finish_wave(from_centre, wave)
+                    kink, near, far = raise_to_cubes(wave, gate)
             nc.scalar.copy(out=base_grouped[:], in_=base_raw[:].rearrange("p t o -> p o t"))
-            nc.vector.quantize_mx(
-                out=w_codes[:, MISH, :].bitcast(FP8X4),
-                scales=w_scales[:, MISH, :],
-                in_=base_grouped[:].rearrange("p o t -> p (o t)"),
-            )
-
-            mish = early.tile([P, ALL], BF16, tag="mish", align_bytes=64)
-            nc.vector.tensor_tensor(out=mish[:], in0=v[:], in1=gate[:], op=ALU.mult)
-            nc.vector.quantize_mx(out=mish_codes[:].bitcast(FP8X4), scales=mish_scales[:], in_=mish[:])
 
         def store(c, acc):
             for m in range(TILES_PER_CHUNK):
@@ -223,9 +223,15 @@ def tile_net_pa_kernel(tc, h1, coef2, sb2, sp2, b2, out):
 
         with tc.tile_pool(name="basis", bufs=1) as basis:
             for c in range(CHUNKS):
+                chunk_gate = gate
+                chunk_below, chunk_wave = below, wave
+                if c + 1 < CHUNKS:
+                    clipped, capped = clip(c + 1)
+                    below, from_centre, wave, gate = fold_waves(clipped, capped)
+
                 cell = basis.tile([P, CHUNK], BF16)
                 nc.vector.tensor_scalar(
-                    out=cell[:], in0=below[:], scalar1=ROUND, scalar2=ROUND, op0=ALU.add, op1=ALU.subtract
+                    out=cell[:], in0=chunk_below[:], scalar1=ROUND, scalar2=ROUND, op0=ALU.add, op1=ALU.subtract
                 )
                 quarter = basis.tile([P, COMBS, CHUNK], BF16)
                 for row, r in enumerate(COMB_OF_ROW):
@@ -235,7 +241,7 @@ def tile_net_pa_kernel(tc, h1, coef2, sb2, sp2, b2, out):
                     )
 
                 nc.vector.scalar_tensor_tensor(
-                    out=kink[:], in0=wave[:], scalar=1.0, in1=kink[:], op0=ALU.subtract, op1=ALU.mult
+                    out=kink[:], in0=chunk_wave[:], scalar=1.0, in1=kink[:], op0=ALU.subtract, op1=ALU.mult
                 )
                 periodic = basis.tile([P, COMBS, CHUNK], BF16)
                 nc.vector.scalar_tensor_tensor(
@@ -247,8 +253,8 @@ def tile_net_pa_kernel(tc, h1, coef2, sb2, sp2, b2, out):
                 )
 
                 if c + 1 < CHUNKS:
-                    below, wave = fold_waves(c + 1)
-                    kink, near, far = raise_to_cubes(wave)
+                    finish_wave(from_centre, wave)
+                    kink, near, far = raise_to_cubes(wave, gate)
 
                 if c > 0:
                     store(c - 1, acc)
@@ -269,9 +275,6 @@ def tile_net_pa_kernel(tc, h1, coef2, sb2, sp2, b2, out):
                             start=first,
                             stop=last,
                         )
-
-                words = slice(c * CHUNK_WORDS, (c + 1) * CHUNK_WORDS)
-                multiply(mish_codes[:, words], mish_scales[:, words], MISH, True, False)
 
                 for n in range(WINDOWS):
                     rows_used = [row for row in range(COMBS) if COMB_OF_ROW[row] + COMBS * n < BASIS]
@@ -294,5 +297,20 @@ def tile_net_pa_kernel(tc, h1, coef2, sb2, sp2, b2, out):
                     )
                     for row in rows_used:
                         g = COMB_OF_ROW[row] + COMBS * n
-                        multiply(codes[:, row, :], scales[:, row, :], g, False, g == BASIS - 1)
+                        multiply(codes[:, row, :], scales[:, row, :], g, g == COMB_OF_ROW[0], False)
+
+                if c == 0:
+                    nc.vector.quantize_mx(
+                        out=w_codes[:, MISH, :].bitcast(FP8X4),
+                        scales=w_scales[:, MISH, :],
+                        in_=base_grouped[:].rearrange("p o t -> p (o t)"),
+                    )
+                mish = gates.tile([P, CHUNK], BF16, align_bytes=64)
+                nc.vector.tensor_tensor(
+                    out=mish[:], in0=v[:, c * CHUNK : (c + 1) * CHUNK], in1=chunk_gate[:], op=ALU.mult
+                )
+                codes = ring.tile([P, CHUNK_WORDS], U32, name="mish_codes", align_bytes=64)
+                scales = ring.tile([P, CHUNK_WORDS], U8, name="mish_scales", align_bytes=64)
+                nc.vector.quantize_mx(out=codes[:].bitcast(FP8X4), scales=scales[:], in_=mish[:])
+                multiply(codes, scales, MISH, False, True)
             store(CHUNKS - 1, acc)

@@ -184,11 +184,9 @@ def tile_net_pa_kernel(tc, h1, coef2, sb2, sp2, b2, out):
                     bank = psum.tile([P, GPSIMD_FIRST_G, O_BLOCK, PACK], BF16, tag="turn", bufs=4)
                     for u in range(2):
                         nc.tensor.matmul(
-                            out=bank[:, :, :, 2 * u : 2 * u + 2].rearrange("p g o e -> p o g e"),
+                            out=bank[:, :, :, 2 * u : 2 * u + 2].rearrange("p g o e -> p e o g"),
                             lhsT=identity_bf[:],
-                            rhs=coef[:, 2 * u : 2 * u + 2, o : o + O_BLOCK, 0:GPSIMD_FIRST_G].rearrange(
-                                "p e o g -> p o g e"
-                            ),
+                            rhs=coef[:, 2 * u : 2 * u + 2, o : o + O_BLOCK, 0:GPSIMD_FIRST_G],
                             start=True,
                             stop=True,
                         )

@@ -62,6 +62,8 @@ def tile_net_pa_kernel(tc, h1, coef2, sb2, sp2, b2, out):
         tc.psum_pool(name="psum", bufs=2) as psum,
     ):
         v = keep.tile([P, ALL], BF16, align_bytes=64)
+        all_clipped = keep.tile([P, ALL], BF16)
+        all_capped = keep.tile([P, ALL], BF16)
         bias = keep.tile([P, OUTPUTS], BF16)
         w_codes = keep.tile([P, BRANCHES, OUTPUTS], U32, align_bytes=64)
         w_scales = keep.tile([P, BRANCHES, OUTPUTS], U8, align_bytes=64)
@@ -69,27 +71,26 @@ def tile_net_pa_kernel(tc, h1, coef2, sb2, sp2, b2, out):
         base_grouped = keep.tile([P, OUTPUTS, PACK], BF16, align_bytes=64)
 
         def clip(c):
-            v_chunk = v[:, c * CHUNK : (c + 1) * CHUNK]
-            clipped = waves.tile([P, CHUNK], BF16)
+            part = slice(c * CHUNK, (c + 1) * CHUNK)
             nc.vector.tensor_scalar(
-                out=clipped[:], in0=v_chunk, scalar1=-V_EDGE, scalar2=V_EDGE, op0=ALU.max, op1=ALU.min
+                out=all_clipped[:, part], in0=v[:, part], scalar1=-V_EDGE, scalar2=V_EDGE, op0=ALU.max, op1=ALU.min
             )
-            capped = gates.tile([P, CHUNK], BF16)
-            nc.vector.tensor_scalar_min(out=capped[:], in0=v_chunk, scalar1=V_CAP)
-            return clipped, capped
+            nc.vector.tensor_scalar_min(out=all_capped[:, part], in0=v[:, part], scalar1=V_CAP)
 
-        def fold_waves(clipped, capped):
+        def fold_waves(c):
+            clipped = all_clipped[:, c * CHUNK : (c + 1) * CHUNK]
+            capped = all_capped[:, c * CHUNK : (c + 1) * CHUNK]
             below = waves.tile([P, CHUNK], F32)
-            nc.scalar.activation(out=below[:], in_=clipped[:], func=ACT.Identity, scale=2.5, bias=7.5)
-            from_centre = waves.tile([P, CHUNK], F32)
+            nc.scalar.activation(out=below[:], in_=clipped, func=ACT.Identity, scale=2.5, bias=7.5)
+            from_centre = waves.tile([P, CHUNK], F32, bufs=1)
             wave = waves.tile([P, 2, CHUNK], F32)
-            nc.scalar.activation(out=from_centre[:], in_=clipped[:], func=ACT.Abs, scale=2.5)
-            nc.scalar.activation(out=wave[:, 1, :], in_=clipped[:], func=ACT.Abs, scale=2.5, bias=-1.0)
+            nc.scalar.activation(out=from_centre[:], in_=clipped, func=ACT.Abs, scale=2.5)
+            nc.scalar.activation(out=wave[:, 1, :], in_=clipped, func=ACT.Abs, scale=2.5, bias=-1.0)
             nc.scalar.activation(out=wave[:, 0, :], in_=from_centre[:], func=ACT.Abs, bias=-6.0)
             nc.scalar.activation(out=wave[:, 1, :], in_=wave[:, 1, :], func=ACT.Abs, bias=-4.0)
             nc.scalar.activation(out=wave[:], in_=wave[:], func=ACT.Abs, bias=-2.0)
             gate = gates.tile([P, CHUNK], F32)
-            nc.scalar.activation(out=gate[:], in_=capped[:], func=ACT.Exp)
+            nc.scalar.activation(out=gate[:], in_=capped, func=ACT.Exp)
             return below, from_centre, wave, gate
 
         def finish_wave(from_centre, wave):
@@ -133,9 +134,9 @@ def tile_net_pa_kernel(tc, h1, coef2, sb2, sp2, b2, out):
                     )
                 return coef_raw
 
-            load_h1(0)
             gain = early.tile([P, PACK, OUTPUTS], BF16)
             nc.sync.dma_start(out=gain[:].rearrange("p (u e) o -> p u (e o)", u=2), in_=words_on_partitions(sp2))
+            load_h1(0)
             coef_pieces = [load_coef(0)]
             for c in range(1, CHUNKS):
                 load_h1(c)
@@ -154,7 +155,8 @@ def tile_net_pa_kernel(tc, h1, coef2, sb2, sp2, b2, out):
             masks.make_identity(nc, identity[:])
             h1_words = h1_rows[:].bitcast(F32)
             v_words = v[:].bitcast(F32).rearrange("p (c m b u) -> p c m b u", c=CHUNKS, m=TILES_PER_CHUNK, u=2)
-            for c in range(CHUNKS):
+
+            def turn_h1(c):
                 turned = psum.tile([P, TILES_PER_CHUNK, 2, P], F32, tag="turn", bufs=4)
                 for m in range(TILES_PER_CHUNK):
                     for u in range(2):
@@ -165,8 +167,11 @@ def tile_net_pa_kernel(tc, h1, coef2, sb2, sp2, b2, out):
                         )
                 nc.scalar.copy(out=v_words[:, c], in_=turned[:].rearrange("p m u b -> p m b u"))
 
-            clipped, capped = clip(0)
-            below, from_centre, wave, gate = fold_waves(clipped, capped)
+            turn_h1(0)
+            clip(0)
+            below, from_centre, wave, gate = fold_waves(0)
+            for c in range(1, CHUNKS):
+                turn_h1(c)
 
             for piece in range(O_PIECES):
                 columns = slice(piece * O_PIECE, (piece + 1) * O_PIECE)
@@ -199,6 +204,9 @@ def tile_net_pa_kernel(tc, h1, coef2, sb2, sp2, b2, out):
                         .to_broadcast([P, GPSIMD_FIRST_G, O_BLOCK * PACK]),
                         op=ALU.mult,
                     )
+                    if piece == 0 and o == 4 * O_BLOCK:
+                        finish_wave(from_centre, wave)
+                        kink, near, far = raise_to_cubes(wave, gate)
                 if piece + 2 < O_PIECES:
                     coef_pieces.append(load_coef(piece + 2))
                 for g in range(BASIS):
@@ -207,9 +215,8 @@ def tile_net_pa_kernel(tc, h1, coef2, sb2, sp2, b2, out):
                         scales=w_scales[:, g, columns],
                         in_=w_grouped[:, g].rearrange("p o t -> p (o t)"),
                     )
-                if piece == 0:
-                    finish_wave(from_centre, wave)
-                    kink, near, far = raise_to_cubes(wave, gate)
+                if piece > 0:
+                    clip(piece)
             nc.scalar.copy(out=base_grouped[:], in_=base_raw[:].rearrange("p t o -> p o t"))
 
         def store(c, acc):
@@ -219,17 +226,26 @@ def tile_net_pa_kernel(tc, h1, coef2, sb2, sp2, b2, out):
                 row0 = (c * TILES_PER_CHUNK + m) * P
                 nc.sync.dma_start(out=out[row0 : row0 + P, :], in_=result[:])
 
+        next_waves = fold_waves(1)
         with tc.tile_pool(name="basis", bufs=1) as basis:
             for c in range(CHUNKS):
-                chunk_gate = gate
-                chunk_below, chunk_wave = below, wave
+                chunk_below, chunk_wave, chunk_gate = below, wave, gate
+                chunk_kink, chunk_near, chunk_far = kink, near, far
                 if c + 1 < CHUNKS:
-                    clipped, capped = clip(c + 1)
-                    below, from_centre, wave, gate = fold_waves(clipped, capped)
+                    below, from_centre, wave, gate = next_waves
 
+
+                nc.vector.scalar_tensor_tensor(
+                    out=chunk_kink[:], in0=chunk_wave[:], scalar=1.0, in1=chunk_kink[:], op0=ALU.subtract, op1=ALU.mult
+                )
                 cell = basis.tile([P, CHUNK], BF16)
                 nc.vector.tensor_scalar(
                     out=cell[:], in0=chunk_below[:], scalar1=ROUND, scalar2=ROUND, op0=ALU.add, op1=ALU.subtract
+                )
+                periodic = basis.tile([P, COMBS, CHUNK], BF16)
+                nc.vector.scalar_tensor_tensor(
+                    out=periodic[:, 0:2, :], in0=chunk_kink[:], scalar=0.0, in1=chunk_near[:], op0=ALU.max,
+                    op1=ALU.subtract, reverse1=True,
                 )
                 quarter = basis.tile([P, COMBS, CHUNK], BF16)
                 for row, r in enumerate(COMB_OF_ROW):
@@ -237,29 +253,35 @@ def tile_net_pa_kernel(tc, h1, coef2, sb2, sp2, b2, out):
                         out=quarter[:, row, :], in0=cell[:], scalar1=0.25, scalar2=-(r + 1.5) / 4.0,
                         op0=ALU.mult, op1=ALU.add,
                     )
-
-                nc.vector.scalar_tensor_tensor(
-                    out=kink[:], in0=chunk_wave[:], scalar=1.0, in1=kink[:], op0=ALU.subtract, op1=ALU.mult
-                )
-                periodic = basis.tile([P, COMBS, CHUNK], BF16)
-                nc.vector.scalar_tensor_tensor(
-                    out=periodic[:, 0:2, :], in0=kink[:], scalar=0.0, in1=near[:], op0=ALU.max, op1=ALU.subtract,
-                    reverse1=True,
-                )
-                nc.vector.scalar_tensor_tensor(
-                    out=periodic[:, 2:4, :], in0=kink[:], scalar=0.0, in1=far[:], op0=ALU.min, op1=ALU.add
-                )
-
                 if c + 1 < CHUNKS:
                     finish_wave(from_centre, wave)
                     kink, near, far = raise_to_cubes(wave, gate)
+                if c + 2 < CHUNKS:
+                    next_waves = fold_waves(c + 2)
+                nc.vector.scalar_tensor_tensor(
+                    out=periodic[:, 2:4, :], in0=chunk_kink[:], scalar=0.0, in1=chunk_far[:], op0=ALU.min, op1=ALU.add
+                )
 
-                if c > 0:
-                    store(c - 1, acc)
-                acc = [
-                    psum.tile([P, OUTPUTS], F32, name="acc", bufs=2 * TILES_PER_CHUNK)
-                    for m in range(TILES_PER_CHUNK)
-                ]
+                rows_of = [[row for row in range(COMBS) if COMB_OF_ROW[row] + COMBS * n < BASIS] for n in range(WINDOWS)]
+                insides = []
+                slabs = []
+
+                def find_window(n):
+                    count = len(rows_of[n])
+                    inside = basis.tile([P, COMBS, CHUNK], BF16, bufs=2)
+                    nc.vector.tensor_scalar(
+                        out=inside[:, 0:count, :], in0=quarter[:, 0:count, :], scalar1=ROUND, scalar2=ROUND + n,
+                        op0=ALU.add, op1=ALU.is_equal,
+                    )
+                    insides.append(inside)
+
+                def cut_out(n):
+                    count = len(rows_of[n])
+                    slab = basis.tile([P, COMBS, CHUNK], BF16, align_bytes=64, bufs=2)
+                    nc.vector.tensor_tensor(
+                        out=slab[:, 0:count, :], in0=periodic[:, 0:count, :], in1=insides[n][:, 0:count, :], op=ALU.mult
+                    )
+                    slabs.append(slab)
 
                 def multiply(codes, scales, branch, first, last):
                     for m in range(TILES_PER_CHUNK):
@@ -274,41 +296,47 @@ def tile_net_pa_kernel(tc, h1, coef2, sb2, sp2, b2, out):
                             stop=last,
                         )
 
-                for n in range(WINDOWS):
-                    rows_used = [row for row in range(COMBS) if COMB_OF_ROW[row] + COMBS * n < BASIS]
-                    count = len(rows_used)
-                    inside = basis.tile([P, COMBS, CHUNK], BF16, bufs=2)
-                    nc.vector.tensor_scalar(
-                        out=inside[:, 0:count, :], in0=quarter[:, 0:count, :], scalar1=ROUND, scalar2=ROUND + n,
-                        op0=ALU.add, op1=ALU.is_equal,
-                    )
-                    slabs = basis.tile([P, COMBS, CHUNK], BF16, align_bytes=64, bufs=2)
-                    nc.vector.tensor_tensor(
-                        out=slabs[:, 0:count, :], in0=periodic[:, 0:count, :], in1=inside[:, 0:count, :], op=ALU.mult
-                    )
+                def quantise_and_multiply(n):
+                    count = len(rows_of[n])
                     codes = ring.tile([P, COMBS, CHUNK_WORDS], U32, align_bytes=64, bufs=3)
                     scales = ring.tile([P, COMBS, CHUNK_WORDS], U8, align_bytes=64, bufs=3)
                     nc.vector.quantize_mx(
                         out=codes[:, 0:count, :].rearrange("p r w -> p (r w)").bitcast(FP8X4),
                         scales=scales[:, 0:count, :].rearrange("p r w -> p (r w)"),
-                        in_=slabs[:, 0:count, :].rearrange("p r k -> p (r k)"),
+                        in_=slabs[n][:, 0:count, :].rearrange("p r k -> p (r k)"),
                     )
-                    for row in rows_used:
+                    for row in rows_of[n]:
                         g = COMB_OF_ROW[row] + COMBS * n
-                        multiply(codes[:, row, :], scales[:, row, :], g, g == COMB_OF_ROW[0], False)
+                        multiply(codes[:, row, :], scales[:, row, :], g, g == 0, g == BASIS - 1)
 
-                if c == 0:
+                find_window(0)
+                if c > 0:
+                    store(c - 1, acc)
+                else:
                     nc.vector.quantize_mx(
                         out=w_codes[:, MISH, :].bitcast(FP8X4),
                         scales=w_scales[:, MISH, :],
                         in_=base_grouped[:].rearrange("p o t -> p (o t)"),
                     )
+                acc = [
+                    psum.tile([P, OUTPUTS], F32, name="acc", bufs=2 * TILES_PER_CHUNK)
+                    for m in range(TILES_PER_CHUNK)
+                ]
+                find_window(1)
+                cut_out(0)
                 mish = gates.tile([P, CHUNK], BF16, align_bytes=64)
                 nc.vector.tensor_tensor(
                     out=mish[:], in0=v[:, c * CHUNK : (c + 1) * CHUNK], in1=chunk_gate[:], op=ALU.mult
                 )
-                codes = ring.tile([P, CHUNK_WORDS], U32, name="mish_codes", align_bytes=64)
-                scales = ring.tile([P, CHUNK_WORDS], U8, name="mish_scales", align_bytes=64)
-                nc.vector.quantize_mx(out=codes[:].bitcast(FP8X4), scales=scales[:], in_=mish[:])
-                multiply(codes, scales, MISH, False, True)
+                quantise_and_multiply(0)
+                for n in range(1, WINDOWS):
+                    cut_out(n)
+                    if n + 1 < WINDOWS:
+                        find_window(n + 1)
+                    else:
+                        mish_codes = ring.tile([P, CHUNK_WORDS], U32, align_bytes=64)
+                        mish_scales = ring.tile([P, CHUNK_WORDS], U8, align_bytes=64)
+                        nc.vector.quantize_mx(out=mish_codes[:].bitcast(FP8X4), scales=mish_scales[:], in_=mish[:])
+                        multiply(mish_codes, mish_scales, MISH, False, False)
+                    quantise_and_multiply(n)
             store(CHUNKS - 1, acc)

@@ -20,7 +20,6 @@ FLOPS = 2 * BATCH * OUTPUTS * FEATURES * BRANCHES
 
 COMBS = 4
 WINDOWS = 4
-COMB_OF_ROW = (0, 3, 2, 1)
 
 ROW_TILES = BATCH // P
 TILES_PER_CHUNK = 2
@@ -31,14 +30,17 @@ ALL = CHUNKS * CHUNK
 
 O_PIECE = 128
 O_PIECES = OUTPUTS // O_PIECE
+O_PAIR = 2 * O_PIECE
 GPSIMD_FIRST_G = 11
-O_BLOCK = 16
+O_BLOCK = 22
 
 ROUND = 12582912.0
+CELL_BASE = 160.0
 V_EDGE = 3.25
 V_CAP = 20.0
-ROOT_TWO_THIRDS = math.sqrt(2.0 / 3.0)
+ROOT_THIRD = math.sqrt(1.0 / 3.0)
 LOG_SIXTH = math.log(1.0 / 6.0)
+NEAREST = 2.0**-10
 SPECK = 2.0**-60
 
 
@@ -48,15 +50,15 @@ def half_of_features(matrix, u):
 
 
 def words_on_partitions(matrix):
-    return matrix.rearrange("(u p e) n -> p u (e n)", u=2, e=2)
+    return matrix.rearrange("(u p e) n -> p u e n", u=2, e=2)
 
 
 def tile_net_pa_kernel(tc, h1, coef2, sb2, sp2, b2, out):
     nc = tc.nc
     with (
+        tc.manual_schedule(engines={mybir.EngineType.DVE, mybir.EngineType.Activation}),
         tc.tile_pool(name="keep", bufs=1) as keep,
         tc.tile_pool(name="waves", bufs=2) as waves,
-        tc.tile_pool(name="cubes", bufs=2) as cubes,
         tc.tile_pool(name="gates", bufs=2) as gates,
         tc.tile_pool(name="ring", bufs=2) as ring,
         tc.psum_pool(name="psum", bufs=2) as psum,
@@ -79,80 +81,89 @@ def tile_net_pa_kernel(tc, h1, coef2, sb2, sp2, b2, out):
 
         def fold_waves(c):
             clipped = all_clipped[:, c * CHUNK : (c + 1) * CHUNK]
-            capped = all_capped[:, c * CHUNK : (c + 1) * CHUNK]
-            below = waves.tile([P, CHUNK], F32)
-            nc.scalar.activation(out=below[:], in_=clipped, func=ACT.Identity, scale=2.5, bias=7.5)
-            from_centre = waves.tile([P, CHUNK], F32, bufs=1)
+            from_8 = waves.tile([P, CHUNK], F32, bufs=1)
             wave = waves.tile([P, 2, CHUNK], F32)
-            nc.scalar.activation(out=from_centre[:], in_=clipped, func=ACT.Abs, scale=2.5)
+            nc.scalar.activation(out=from_8[:], in_=clipped, func=ACT.Abs, scale=2.5)
+            nc.scalar.activation(out=wave[:, 0, :], in_=from_8[:], func=ACT.Abs, bias=-4.0)
             nc.scalar.activation(out=wave[:, 1, :], in_=clipped, func=ACT.Abs, scale=2.5, bias=-1.0)
-            nc.scalar.activation(out=wave[:, 0, :], in_=from_centre[:], func=ACT.Abs, bias=-6.0)
             nc.scalar.activation(out=wave[:, 1, :], in_=wave[:, 1, :], func=ACT.Abs, bias=-4.0)
             nc.scalar.activation(out=wave[:], in_=wave[:], func=ACT.Abs, bias=-2.0)
-            gate = gates.tile([P, CHUNK], F32)
-            nc.scalar.activation(out=gate[:], in_=capped, func=ACT.Exp)
-            return below, from_centre, wave, gate
+            far = waves.tile([P, 2, CHUNK], F32)
+            nc.scalar.activation(out=far[:, 1, :], in_=wave[:, 0, :], func=ACT.Abs, bias=-1.0)
+            nc.scalar.activation(out=far[:, 0, :], in_=far[:, 1, :], func=ACT.Abs, scale=-1.0, bias=1.0)
+            cell = waves.tile([P, CHUNK], BF16)
+            nc.scalar.activation(out=cell[:], in_=clipped, func=ACT.Identity, scale=2.5, bias=CELL_BASE + 7.5)
+            return from_8, wave, far, cell
 
-        def finish_wave(from_centre, wave):
-            nc.vector.tensor_tensor(out=wave[:, 0, :], in0=from_centre[:], in1=wave[:, 0, :], op=ALU.min)
-
-        def raise_to_cubes(wave, gate):
-            kink = cubes.tile([P, 2, CHUNK], F32)
-            near = cubes.tile([P, 2, CHUNK], F32)
-            far = cubes.tile([P, 2, CHUNK], F32)
-            nc.scalar.activation(
-                out=kink[:], in_=wave[:], func=ACT.Square, scale=ROOT_TWO_THIRDS, bias=-ROOT_TWO_THIRDS
+        def mend_tiny(from_8, far):
+            nc.vector.scalar_tensor_tensor(
+                out=far[:, 0, :], in0=far[:, 0, :], scalar=NEAREST, in1=from_8[:], op0=ALU.max, op1=ALU.min
             )
-            nc.scalar.activation(out=far[:, 1, :], in_=wave[:, 1, :], func=ACT.Abs, scale=-1.0, bias=2.0)
-            nc.scalar.activation(out=near[:], in_=wave[:], func=ACT.Ln, bias=SPECK)
-            nc.scalar.activation(out=far[:, 0, :], in_=wave[:, 0, :], func=ACT.Ln, scale=-1.0, bias=2.0)
-            nc.scalar.activation(out=far[:, 1, :], in_=far[:, 1, :], func=ACT.Ln, bias=SPECK)
+
+        def slope_of(wave):
+            slope = waves.tile([P, 2, CHUNK], F32)
+            nc.scalar.activation(out=slope[:], in_=wave[:], func=ACT.Square, scale=ROOT_THIRD, bias=-ROOT_THIRD)
+            nc.scalar.activation(out=slope[:], in_=slope[:], func=ACT.Identity, scale=-1.0, bias=1.0)
+            return slope
+
+        def cube(c, far):
+            gate = gates.tile([P, CHUNK], F32)
+            nc.scalar.activation(out=gate[:], in_=all_capped[:, c * CHUNK : (c + 1) * CHUNK], func=ACT.Exp)
+            nc.scalar.activation(out=far[:], in_=far[:], func=ACT.Ln, bias=SPECK)
             nc.scalar.activation(out=gate[:], in_=gate[:], func=ACT.Ln, bias=1.0)
-            nc.scalar.activation(out=near[:], in_=near[:], func=ACT.Exp, scale=3.0, bias=LOG_SIXTH)
             nc.scalar.activation(out=far[:], in_=far[:], func=ACT.Exp, scale=3.0, bias=LOG_SIXTH)
             nc.scalar.activation(out=gate[:], in_=gate[:], func=ACT.Tanh)
-            return kink, near, far
+            return gate
 
         with (
             tc.tile_pool(name="early", bufs=1) as early,
-            tc.tile_pool(name="stream", bufs=2) as stream,
+            tc.tile_pool(name="stream", bufs=3) as stream,
         ):
-            h1_rows = early.tile([P, ROW_TILES, FEATURES], BF16, tag="h1")
+            h1_rows = early.tile([P, ROW_TILES, FEATURES], BF16)
             h1_by_tile = h1.rearrange("(m p) i -> p m i", p=P)
+            gain = early.tile([P, PACK, OUTPUTS], BF16)
 
             def load_h1(c):
                 tiles = slice(c * TILES_PER_CHUNK, (c + 1) * TILES_PER_CHUNK)
                 nc.sync.dma_start(out=h1_rows[:, tiles, :], in_=h1_by_tile[:, tiles, :])
 
-            def load_coef(piece):
-                coef_raw = stream.tile([P, PACK, O_PIECE * BASIS], BF16)
-                columns = slice(piece * O_PIECE, (piece + 1) * O_PIECE)
+            def load_gain(first, last):
                 for u in range(2):
                     nc.sync.dma_start(
-                        out=coef_raw[:, 2 * u : 2 * u + 2, :],
-                        in_=half_of_features(coef2, u)[:, columns, :].rearrange("(p e) o g -> p e (o g)", e=2),
+                        out=gain[:, 2 * u : 2 * u + 2, first:last], in_=words_on_partitions(sp2)[:, u, :, first:last]
                     )
+
+            def load_coef(piece, parts):
+                coef_raw = stream.tile([P, PACK, O_PIECE * BASIS], BF16)
+                width = O_PIECE // parts
+                for part in range(parts):
+                    for u in range(2):
+                        first = piece * O_PIECE + part * width
+                        nc.sync.dma_start(
+                            out=coef_raw[:, 2 * u : 2 * u + 2, part * width * BASIS : (part + 1) * width * BASIS],
+                            in_=half_of_features(coef2, u)[:, first : first + width, :].rearrange(
+                                "(p e) o g -> p e (o g)", e=2
+                            ),
+                        )
                 return coef_raw
 
-            gain = early.tile([P, PACK, OUTPUTS], BF16)
-            nc.sync.dma_start(out=gain[:].rearrange("p (u e) o -> p u (e o)", u=2), in_=words_on_partitions(sp2))
             load_h1(0)
-            coef_pieces = [load_coef(0)]
+            load_gain(0, O_PIECE)
+            coef_pieces = [load_coef(0, 2)]
+            load_gain(O_PIECE, OUTPUTS)
+            coef_pieces.append(load_coef(1, 1))
             for c in range(1, CHUNKS):
                 load_h1(c)
-            coef_pieces.append(load_coef(1))
-            nc.sync.dma_start(
-                out=base_raw[:].rearrange("p (u e) o -> p u (e o)", u=2), in_=words_on_partitions(sb2)
-            )
+            coef_pieces.append(load_coef(2, 1))
+            for u in range(2):
+                nc.sync.dma_start(out=base_raw[:, 2 * u : 2 * u + 2, :], in_=words_on_partitions(sb2)[:, u])
             nc.sync.dma_start(out=bias[:], in_=b2.partition_broadcast(P))
-
-            gain_grouped = early.tile([P, OUTPUTS, PACK], BF16)
-            nc.vector.tensor_copy(out=gain_grouped[:], in_=gain[:].rearrange("p t o -> p o t"))
-            identity_bf = early.tile([P, P], BF16)
-            masks.make_identity(nc, identity_bf[:])
 
             identity = early.tile([P, P], F32)
             masks.make_identity(nc, identity[:])
+            identity_bf = early.tile([P, P], BF16)
+            masks.make_identity(nc, identity_bf[:])
+
             h1_words = h1_rows[:].bitcast(F32)
             v_words = v[:].bitcast(F32).rearrange("p (c m b u) -> p c m b u", c=CHUNKS, m=TILES_PER_CHUNK, u=2)
 
@@ -167,57 +178,79 @@ def tile_net_pa_kernel(tc, h1, coef2, sb2, sp2, b2, out):
                         )
                 nc.scalar.copy(out=v_words[:, c], in_=turned[:].rearrange("p m u b -> p m b u"))
 
+            gain_grouped = early.tile([P, OUTPUTS, PACK], BF16)
+
+            def regroup_gain(first, last):
+                nc.vector.tensor_copy(
+                    out=gain_grouped[:, first:last], in_=gain[:, :, first:last].rearrange("p t o -> p o t")
+                )
+
             turn_h1(0)
             clip(0)
-            below, from_centre, wave, gate = fold_waves(0)
-            for c in range(1, CHUNKS):
-                turn_h1(c)
+            from_8, wave, far, cell = fold_waves(0)
+            regroup_gain(0, O_PIECE)
 
             for piece in range(O_PIECES):
-                columns = slice(piece * O_PIECE, (piece + 1) * O_PIECE)
                 coef = coef_pieces[piece][:].rearrange("p t (o g) -> p t o g", g=BASIS)
-                w_grouped = early.tile([P, BASIS, O_PIECE, PACK], BF16, align_bytes=64)
+                in_pair = piece % 2 * O_PIECE
+                if in_pair == 0:
+                    w_grouped = early.tile([P, GPSIMD_FIRST_G, O_PAIR, PACK], BF16, align_bytes=64)
+                    w_gpsimd = early.tile([P, BASIS - GPSIMD_FIRST_G, O_PAIR, PACK], BF16, align_bytes=64)
 
                 for g in range(GPSIMD_FIRST_G, BASIS):
                     nc.gpsimd.tensor_tensor(
-                        out=w_grouped[:, g],
+                        out=w_gpsimd[:, g - GPSIMD_FIRST_G, in_pair : in_pair + O_PIECE],
                         in0=coef[:, :, :, g].rearrange("p t o -> p o t"),
-                        in1=gain_grouped[:, columns],
+                        in1=gain_grouped[:, piece * O_PIECE : (piece + 1) * O_PIECE],
                         op=ALU.mult,
                     )
                 for o in range(0, O_PIECE, O_BLOCK):
-                    bank = psum.tile([P, GPSIMD_FIRST_G, O_BLOCK, PACK], BF16, tag="turn", bufs=4)
+                    width = min(O_BLOCK, O_PIECE - o)
+                    bank = psum.tile([P, GPSIMD_FIRST_G, width, PACK], BF16, tag="turn", bufs=4)
                     for u in range(2):
                         nc.tensor.matmul(
                             out=bank[:, :, :, 2 * u : 2 * u + 2].rearrange("p g o e -> p e o g"),
                             lhsT=identity_bf[:],
-                            rhs=coef[:, 2 * u : 2 * u + 2, o : o + O_BLOCK, 0:GPSIMD_FIRST_G],
+                            rhs=coef[:, 2 * u : 2 * u + 2, o : o + width, 0:GPSIMD_FIRST_G],
                             start=True,
                             stop=True,
                         )
-                    block_gain = gain_grouped[:, piece * O_PIECE + o : piece * O_PIECE + o + O_BLOCK]
+                    block_gain = gain_grouped[:, piece * O_PIECE + o : piece * O_PIECE + o + width]
                     nc.vector.tensor_tensor(
-                        out=w_grouped[:, 0:GPSIMD_FIRST_G, o : o + O_BLOCK].rearrange("p g o t -> p g (o t)"),
+                        out=w_grouped[:, :, in_pair + o : in_pair + o + width].rearrange("p g o t -> p g (o t)"),
                         in0=bank[:].rearrange("p g o t -> p g (o t)"),
                         in1=block_gain.rearrange("p o t -> p (o t)")
                         .unsqueeze(1)
-                        .to_broadcast([P, GPSIMD_FIRST_G, O_BLOCK * PACK]),
+                        .to_broadcast([P, GPSIMD_FIRST_G, width * PACK]),
                         op=ALU.mult,
                     )
-                    if piece == 0 and o == 4 * O_BLOCK:
-                        finish_wave(from_centre, wave)
-                        kink, near, far = raise_to_cubes(wave, gate)
-                if piece + 2 < O_PIECES:
-                    coef_pieces.append(load_coef(piece + 2))
-                for g in range(BASIS):
-                    nc.vector.quantize_mx(
-                        out=w_codes[:, g, columns].bitcast(FP8X4),
-                        scales=w_scales[:, g, columns],
-                        in_=w_grouped[:, g].rearrange("p o t -> p (o t)"),
+                if piece + 3 < O_PIECES:
+                    coef_pieces.append(load_coef(piece + 3, 1))
+
+                if piece == 0:
+                    regroup_gain(O_PIECE, OUTPUTS)
+                elif piece == 1:
+                    mend_tiny(from_8, far)
+                    for c in range(1, CHUNKS):
+                        turn_h1(c)
+                    slope = slope_of(wave)
+                    gate = cube(0, far)
+                    nc.gpsimd.tensor_scalar(
+                        out=base_grouped[:], in0=base_raw[:].rearrange("p t o -> p o t"), scalar1=1.0, scalar2=0.0,
+                        op0=ALU.mult, op1=ALU.add,
                     )
-                if piece > 0:
-                    clip(piece)
-            nc.scalar.copy(out=base_grouped[:], in_=base_raw[:].rearrange("p t o -> p o t"))
+                if in_pair > 0:
+                    columns = slice((piece - 1) * O_PIECE, (piece + 1) * O_PIECE)
+                    for g in range(BASIS):
+                        grouped = w_grouped[:, g] if g < GPSIMD_FIRST_G else w_gpsimd[:, g - GPSIMD_FIRST_G]
+                        nc.vector.quantize_mx(
+                            out=w_codes[:, g, columns].bitcast(FP8X4),
+                            scales=w_scales[:, g, columns],
+                            in_=grouped.rearrange("p o t -> p (o t)"),
+                        )
+                if piece == 1:
+                    for c in range(1, CHUNKS):
+                        clip(c)
 
         def store(c, acc):
             for m in range(TILES_PER_CHUNK):
@@ -226,48 +259,36 @@ def tile_net_pa_kernel(tc, h1, coef2, sb2, sp2, b2, out):
                 row0 = (c * TILES_PER_CHUNK + m) * P
                 nc.sync.dma_start(out=out[row0 : row0 + P, :], in_=result[:])
 
-        next_waves = fold_waves(1)
+        next_fold = fold_waves(1)
         with tc.tile_pool(name="basis", bufs=1) as basis:
             for c in range(CHUNKS):
-                chunk_below, chunk_wave, chunk_gate = below, wave, gate
-                chunk_kink, chunk_near, chunk_far = kink, near, far
-                if c + 1 < CHUNKS:
-                    below, from_centre, wave, gate = next_waves
-
+                chunk_wave, chunk_far, chunk_slope, chunk_cell, chunk_gate = wave, far, slope, cell, gate
 
                 nc.vector.scalar_tensor_tensor(
-                    out=chunk_kink[:], in0=chunk_wave[:], scalar=1.0, in1=chunk_kink[:], op0=ALU.subtract, op1=ALU.mult
-                )
-                cell = basis.tile([P, CHUNK], BF16)
-                nc.vector.tensor_scalar(
-                    out=cell[:], in0=chunk_below[:], scalar1=ROUND, scalar2=ROUND, op0=ALU.add, op1=ALU.subtract
-                )
-                periodic = basis.tile([P, COMBS, CHUNK], BF16)
-                nc.vector.scalar_tensor_tensor(
-                    out=periodic[:, 0:2, :], in0=chunk_kink[:], scalar=0.0, in1=chunk_near[:], op0=ALU.max,
-                    op1=ALU.subtract, reverse1=True,
+                    out=chunk_slope[:], in0=chunk_wave[:], scalar=1.0, in1=chunk_slope[:], op0=ALU.subtract,
+                    op1=ALU.mult,
                 )
                 quarter = basis.tile([P, COMBS, CHUNK], BF16)
-                for row, r in enumerate(COMB_OF_ROW):
+                for r in range(COMBS):
                     nc.vector.tensor_scalar(
-                        out=quarter[:, row, :], in0=cell[:], scalar1=0.25, scalar2=-(r + 1.5) / 4.0,
+                        out=quarter[:, r, :], in0=chunk_cell[:], scalar1=0.25, scalar2=-(CELL_BASE + r + 1.5) / 4.0,
                         op0=ALU.mult, op1=ALU.add,
                     )
-                if c + 1 < CHUNKS:
-                    finish_wave(from_centre, wave)
-                    kink, near, far = raise_to_cubes(wave, gate)
-                if c + 2 < CHUNKS:
-                    next_waves = fold_waves(c + 2)
+                periodic = basis.tile([P, COMBS, CHUNK], BF16)
                 nc.vector.scalar_tensor_tensor(
-                    out=periodic[:, 2:4, :], in0=chunk_kink[:], scalar=0.0, in1=chunk_far[:], op0=ALU.min, op1=ALU.add
+                    out=periodic[:, 0:2, :], in0=chunk_slope[:], scalar=0.0, in1=chunk_far[:], op0=ALU.min,
+                    op1=ALU.subtract, reverse1=True,
+                )
+                nc.vector.scalar_tensor_tensor(
+                    out=periodic[:, 2:4, :], in0=chunk_slope[:], scalar=0.0, in1=chunk_far[:], op0=ALU.max, op1=ALU.add
                 )
 
-                rows_of = [[row for row in range(COMBS) if COMB_OF_ROW[row] + COMBS * n < BASIS] for n in range(WINDOWS)]
+                combs_of = [sum(1 for r in range(COMBS) if r + COMBS * n < BASIS) for n in range(WINDOWS)]
                 insides = []
                 slabs = []
 
                 def find_window(n):
-                    count = len(rows_of[n])
+                    count = combs_of[n]
                     inside = basis.tile([P, COMBS, CHUNK], BF16, bufs=2)
                     nc.vector.tensor_scalar(
                         out=inside[:, 0:count, :], in0=quarter[:, 0:count, :], scalar1=ROUND, scalar2=ROUND + n,
@@ -276,7 +297,7 @@ def tile_net_pa_kernel(tc, h1, coef2, sb2, sp2, b2, out):
                     insides.append(inside)
 
                 def cut_out(n):
-                    count = len(rows_of[n])
+                    count = combs_of[n]
                     slab = basis.tile([P, COMBS, CHUNK], BF16, align_bytes=64, bufs=2)
                     nc.vector.tensor_tensor(
                         out=slab[:, 0:count, :], in0=periodic[:, 0:count, :], in1=insides[n][:, 0:count, :], op=ALU.mult
@@ -297,17 +318,17 @@ def tile_net_pa_kernel(tc, h1, coef2, sb2, sp2, b2, out):
                         )
 
                 def quantise_and_multiply(n):
-                    count = len(rows_of[n])
-                    codes = ring.tile([P, COMBS, CHUNK_WORDS], U32, align_bytes=64, bufs=3)
-                    scales = ring.tile([P, COMBS, CHUNK_WORDS], U8, align_bytes=64, bufs=3)
+                    count = combs_of[n]
+                    codes = ring.tile([P, COMBS, CHUNK_WORDS], U32, align_bytes=64)
+                    scales = ring.tile([P, COMBS, CHUNK_WORDS], U8, align_bytes=64)
                     nc.vector.quantize_mx(
                         out=codes[:, 0:count, :].rearrange("p r w -> p (r w)").bitcast(FP8X4),
                         scales=scales[:, 0:count, :].rearrange("p r w -> p (r w)"),
                         in_=slabs[n][:, 0:count, :].rearrange("p r k -> p (r k)"),
                     )
-                    for row in rows_of[n]:
-                        g = COMB_OF_ROW[row] + COMBS * n
-                        multiply(codes[:, row, :], scales[:, row, :], g, g == 0, g == BASIS - 1)
+                    for r in range(count):
+                        g = r + COMBS * n
+                        multiply(codes[:, r, :], scales[:, r, :], g, g == 0, g == BASIS - 1)
 
                 find_window(0)
                 if c > 0:
@@ -322,21 +343,28 @@ def tile_net_pa_kernel(tc, h1, coef2, sb2, sp2, b2, out):
                     psum.tile([P, OUTPUTS], F32, name="acc", bufs=2 * TILES_PER_CHUNK)
                     for m in range(TILES_PER_CHUNK)
                 ]
+                if c + 1 < CHUNKS:
+                    from_8, wave, far, cell = next_fold
+                    mend_tiny(from_8, far)
+                    slope = slope_of(wave)
+                    gate = cube(c + 1, far)
+                if c + 2 < CHUNKS:
+                    next_fold = fold_waves(c + 2)
                 find_window(1)
                 cut_out(0)
+                quantise_and_multiply(0)
+                for n in range(1, WINDOWS - 1):
+                    cut_out(n)
+                    find_window(n + 1)
+                    quantise_and_multiply(n)
                 mish = gates.tile([P, CHUNK], BF16, align_bytes=64)
                 nc.vector.tensor_tensor(
                     out=mish[:], in0=v[:, c * CHUNK : (c + 1) * CHUNK], in1=chunk_gate[:], op=ALU.mult
                 )
-                quantise_and_multiply(0)
-                for n in range(1, WINDOWS):
-                    cut_out(n)
-                    if n + 1 < WINDOWS:
-                        find_window(n + 1)
-                    else:
-                        mish_codes = ring.tile([P, CHUNK_WORDS], U32, align_bytes=64)
-                        mish_scales = ring.tile([P, CHUNK_WORDS], U8, align_bytes=64)
-                        nc.vector.quantize_mx(out=mish_codes[:].bitcast(FP8X4), scales=mish_scales[:], in_=mish[:])
-                        multiply(mish_codes, mish_scales, MISH, False, False)
-                    quantise_and_multiply(n)
+                cut_out(WINDOWS - 1)
+                mish_codes = ring.tile([P, CHUNK_WORDS], U32, align_bytes=64)
+                mish_scales = ring.tile([P, CHUNK_WORDS], U8, align_bytes=64)
+                nc.vector.quantize_mx(out=mish_codes[:].bitcast(FP8X4), scales=mish_scales[:], in_=mish[:])
+                multiply(mish_codes, mish_scales, MISH, False, False)
+                quantise_and_multiply(WINDOWS - 1)
             store(CHUNKS - 1, acc)

@@ -30,14 +30,14 @@ ALL = CHUNKS * CHUNK
 
 O_PIECE = 128
 O_PIECES = OUTPUTS // O_PIECE
-O_PAIR = 2 * O_PIECE
-GPSIMD_FIRST_G = 11
+O_GROUPS = ((0, 1), (2,), (3,))
+GPSIMD_FIRST_G = 10
 O_BLOCK = 22
 
 ROUND = 12582912.0
 CELL_BASE = 160.0
-V_EDGE = 3.25
-V_CAP = 20.0
+V_HIGH = 20.0
+V_LOW = -104.0
 ROOT_THIRD = math.sqrt(1.0 / 3.0)
 LOG_SIXTH = math.log(1.0 / 6.0)
 NEAREST = 2.0**-10
@@ -64,8 +64,8 @@ def tile_net_pa_kernel(tc, h1, coef2, sb2, sp2, b2, out):
         tc.psum_pool(name="psum", bufs=2) as psum,
     ):
         v = keep.tile([P, ALL], BF16, align_bytes=64)
-        all_clipped = keep.tile([P, ALL], BF16)
-        all_capped = keep.tile([P, ALL], BF16)
+        clipped = keep.tile([P, ALL], BF16)
+        cells = keep.tile([P, ALL], BF16)
         bias = keep.tile([P, OUTPUTS], BF16)
         w_codes = keep.tile([P, BRANCHES, OUTPUTS], U32, align_bytes=64)
         w_scales = keep.tile([P, BRANCHES, OUTPUTS], U8, align_bytes=64)
@@ -75,25 +75,29 @@ def tile_net_pa_kernel(tc, h1, coef2, sb2, sp2, b2, out):
         def clip(c):
             part = slice(c * CHUNK, (c + 1) * CHUNK)
             nc.vector.tensor_scalar(
-                out=all_clipped[:, part], in0=v[:, part], scalar1=-V_EDGE, scalar2=V_EDGE, op0=ALU.max, op1=ALU.min
+                out=clipped[:, part], in0=v[:, part], scalar1=V_LOW, scalar2=V_HIGH, op0=ALU.max, op1=ALU.min
             )
-            nc.vector.tensor_scalar_min(out=all_capped[:, part], in0=v[:, part], scalar1=V_CAP)
 
         def fold_waves(c):
-            clipped = all_clipped[:, c * CHUNK : (c + 1) * CHUNK]
+            chunk = clipped[:, c * CHUNK : (c + 1) * CHUNK]
             from_8 = waves.tile([P, CHUNK], F32, bufs=1)
             wave = waves.tile([P, 2, CHUNK], F32)
-            nc.scalar.activation(out=from_8[:], in_=clipped, func=ACT.Abs, scale=2.5)
+            nc.scalar.activation(out=from_8[:], in_=chunk, func=ACT.Abs, scale=2.5)
             nc.scalar.activation(out=wave[:, 0, :], in_=from_8[:], func=ACT.Abs, bias=-4.0)
-            nc.scalar.activation(out=wave[:, 1, :], in_=clipped, func=ACT.Abs, scale=2.5, bias=-1.0)
+            nc.scalar.activation(out=wave[:, 1, :], in_=chunk, func=ACT.Abs, scale=2.5, bias=-1.0)
             nc.scalar.activation(out=wave[:, 1, :], in_=wave[:, 1, :], func=ACT.Abs, bias=-4.0)
             nc.scalar.activation(out=wave[:], in_=wave[:], func=ACT.Abs, bias=-2.0)
             far = waves.tile([P, 2, CHUNK], F32)
             nc.scalar.activation(out=far[:, 1, :], in_=wave[:, 0, :], func=ACT.Abs, bias=-1.0)
             nc.scalar.activation(out=far[:, 0, :], in_=far[:, 1, :], func=ACT.Abs, scale=-1.0, bias=1.0)
-            cell = waves.tile([P, CHUNK], BF16)
-            nc.scalar.activation(out=cell[:], in_=clipped, func=ACT.Identity, scale=2.5, bias=CELL_BASE + 7.5)
-            return from_8, wave, far, cell
+            return from_8, wave, far
+
+        def find_cells(c):
+            part = slice(c * CHUNK, (c + 1) * CHUNK)
+            nc.gpsimd.tensor_scalar(
+                out=cells[:, part], in0=clipped[:, part], scalar1=2.5, scalar2=CELL_BASE + 7.5,
+                op0=ALU.mult, op1=ALU.add,
+            )
 
         def mend_tiny(from_8, far):
             nc.vector.scalar_tensor_tensor(
@@ -108,7 +112,7 @@ def tile_net_pa_kernel(tc, h1, coef2, sb2, sp2, b2, out):
 
         def cube(c, far):
             gate = gates.tile([P, CHUNK], F32)
-            nc.scalar.activation(out=gate[:], in_=all_capped[:, c * CHUNK : (c + 1) * CHUNK], func=ACT.Exp)
+            nc.scalar.activation(out=gate[:], in_=clipped[:, c * CHUNK : (c + 1) * CHUNK], func=ACT.Exp)
             nc.scalar.activation(out=far[:], in_=far[:], func=ACT.Ln, bias=SPECK)
             nc.scalar.activation(out=gate[:], in_=gate[:], func=ACT.Ln, bias=1.0)
             nc.scalar.activation(out=far[:], in_=far[:], func=ACT.Exp, scale=3.0, bias=LOG_SIXTH)
@@ -187,19 +191,22 @@ def tile_net_pa_kernel(tc, h1, coef2, sb2, sp2, b2, out):
 
             turn_h1(0)
             clip(0)
-            from_8, wave, far, cell = fold_waves(0)
+            from_8, wave, far = fold_waves(0)
             regroup_gain(0, O_PIECE)
 
-            for piece in range(O_PIECES):
+            for group, piece in [(group, piece) for group in O_GROUPS for piece in group]:
                 coef = coef_pieces[piece][:].rearrange("p t (o g) -> p t o g", g=BASIS)
-                in_pair = piece % 2 * O_PIECE
-                if in_pair == 0:
-                    w_grouped = early.tile([P, GPSIMD_FIRST_G, O_PAIR, PACK], BF16, align_bytes=64)
-                    w_gpsimd = early.tile([P, BASIS - GPSIMD_FIRST_G, O_PAIR, PACK], BF16, align_bytes=64)
+                in_group = (piece - group[0]) * O_PIECE
+                if in_group == 0:
+                    group_width = len(group) * O_PIECE
+                    w_grouped = early.tile([P, GPSIMD_FIRST_G, group_width, PACK], BF16, align_bytes=64)
+                    w_gpsimd = early.tile(
+                        [P, BASIS - GPSIMD_FIRST_G, group_width, PACK], BF16, align_bytes=64, bufs=2
+                    )
 
                 for g in range(GPSIMD_FIRST_G, BASIS):
                     nc.gpsimd.tensor_tensor(
-                        out=w_gpsimd[:, g - GPSIMD_FIRST_G, in_pair : in_pair + O_PIECE],
+                        out=w_gpsimd[:, g - GPSIMD_FIRST_G, in_group : in_group + O_PIECE],
                         in0=coef[:, :, :, g].rearrange("p t o -> p o t"),
                         in1=gain_grouped[:, piece * O_PIECE : (piece + 1) * O_PIECE],
                         op=ALU.mult,
@@ -217,7 +224,7 @@ def tile_net_pa_kernel(tc, h1, coef2, sb2, sp2, b2, out):
                         )
                     block_gain = gain_grouped[:, piece * O_PIECE + o : piece * O_PIECE + o + width]
                     nc.vector.tensor_tensor(
-                        out=w_grouped[:, :, in_pair + o : in_pair + o + width].rearrange("p g o t -> p g (o t)"),
+                        out=w_grouped[:, :, in_group + o : in_group + o + width].rearrange("p g o t -> p g (o t)"),
                         in0=bank[:].rearrange("p g o t -> p g (o t)"),
                         in1=block_gain.rearrange("p o t -> p (o t)")
                         .unsqueeze(1)
@@ -239,8 +246,8 @@ def tile_net_pa_kernel(tc, h1, coef2, sb2, sp2, b2, out):
                         out=base_grouped[:], in0=base_raw[:].rearrange("p t o -> p o t"), scalar1=1.0, scalar2=0.0,
                         op0=ALU.mult, op1=ALU.add,
                     )
-                if in_pair > 0:
-                    columns = slice((piece - 1) * O_PIECE, (piece + 1) * O_PIECE)
+                if piece == group[-1]:
+                    columns = slice(group[0] * O_PIECE, (piece + 1) * O_PIECE)
                     for g in range(BASIS):
                         grouped = w_grouped[:, g] if g < GPSIMD_FIRST_G else w_gpsimd[:, g - GPSIMD_FIRST_G]
                         nc.vector.quantize_mx(
@@ -251,6 +258,9 @@ def tile_net_pa_kernel(tc, h1, coef2, sb2, sp2, b2, out):
                 if piece == 1:
                     for c in range(1, CHUNKS):
                         clip(c)
+                elif piece == O_PIECES - 1:
+                    for c in range(CHUNKS):
+                        find_cells(c)
 
         def store(c, acc):
             for m in range(TILES_PER_CHUNK):
@@ -259,10 +269,11 @@ def tile_net_pa_kernel(tc, h1, coef2, sb2, sp2, b2, out):
                 row0 = (c * TILES_PER_CHUNK + m) * P
                 nc.sync.dma_start(out=out[row0 : row0 + P, :], in_=result[:])
 
+        acc = None
         next_fold = fold_waves(1)
         with tc.tile_pool(name="basis", bufs=1) as basis:
             for c in range(CHUNKS):
-                chunk_wave, chunk_far, chunk_slope, chunk_cell, chunk_gate = wave, far, slope, cell, gate
+                chunk_wave, chunk_far, chunk_slope, chunk_gate = wave, far, slope, gate
 
                 nc.vector.scalar_tensor_tensor(
                     out=chunk_slope[:], in0=chunk_wave[:], scalar=1.0, in1=chunk_slope[:], op0=ALU.subtract,
@@ -271,8 +282,8 @@ def tile_net_pa_kernel(tc, h1, coef2, sb2, sp2, b2, out):
                 quarter = basis.tile([P, COMBS, CHUNK], BF16)
                 for r in range(COMBS):
                     nc.vector.tensor_scalar(
-                        out=quarter[:, r, :], in0=chunk_cell[:], scalar1=0.25, scalar2=-(CELL_BASE + r + 1.5) / 4.0,
-                        op0=ALU.mult, op1=ALU.add,
+                        out=quarter[:, r, :], in0=cells[:, c * CHUNK : (c + 1) * CHUNK], scalar1=0.25,
+                        scalar2=-(CELL_BASE + r + 1.5) / 4.0, op0=ALU.mult, op1=ALU.add,
                     )
                 periodic = basis.tile([P, COMBS, CHUNK], BF16)
                 nc.vector.scalar_tensor_tensor(
@@ -331,27 +342,26 @@ def tile_net_pa_kernel(tc, h1, coef2, sb2, sp2, b2, out):
                         multiply(codes[:, r, :], scales[:, r, :], g, g == 0, g == BASIS - 1)
 
                 find_window(0)
-                if c > 0:
-                    store(c - 1, acc)
-                else:
+                if c == 0:
                     nc.vector.quantize_mx(
                         out=w_codes[:, MISH, :].bitcast(FP8X4),
                         scales=w_scales[:, MISH, :],
                         in_=base_grouped[:].rearrange("p o t -> p (o t)"),
                     )
+                last_acc = acc
                 acc = [
                     psum.tile([P, OUTPUTS], F32, name="acc", bufs=2 * TILES_PER_CHUNK)
                     for m in range(TILES_PER_CHUNK)
                 ]
+                find_window(1)
+                cut_out(0)
                 if c + 1 < CHUNKS:
-                    from_8, wave, far, cell = next_fold
+                    from_8, wave, far = next_fold
                     mend_tiny(from_8, far)
                     slope = slope_of(wave)
                     gate = cube(c + 1, far)
                 if c + 2 < CHUNKS:
                     next_fold = fold_waves(c + 2)
-                find_window(1)
-                cut_out(0)
                 quantise_and_multiply(0)
                 for n in range(1, WINDOWS - 1):
                     cut_out(n)
@@ -361,6 +371,8 @@ def tile_net_pa_kernel(tc, h1, coef2, sb2, sp2, b2, out):
                 nc.vector.tensor_tensor(
                     out=mish[:], in0=v[:, c * CHUNK : (c + 1) * CHUNK], in1=chunk_gate[:], op=ALU.mult
                 )
+                if c > 0:
+                    store(c - 1, last_acc)
                 cut_out(WINDOWS - 1)
                 mish_codes = ring.tile([P, CHUNK_WORDS], U32, align_bytes=64)
                 mish_scales = ring.tile([P, CHUNK_WORDS], U8, align_bytes=64)

@@ -31,7 +31,7 @@ ALL = CHUNKS * CHUNK
 O_PIECE = 128
 O_PIECES = OUTPUTS // O_PIECE
 O_GROUPS = ((0, 1), (2,), (3,))
-GPSIMD_FIRST_G = 10
+GPSIMD_FIRST_G = 11
 O_BLOCK = 22
 
 ROUND = 12582912.0
@@ -94,7 +94,7 @@ def tile_net_pa_kernel(tc, h1, coef2, sb2, sp2, b2, out):
 
         def find_cells(c):
             part = slice(c * CHUNK, (c + 1) * CHUNK)
-            nc.gpsimd.tensor_scalar(
+            nc.vector.tensor_scalar(
                 out=cells[:, part], in0=clipped[:, part], scalar1=2.5, scalar2=CELL_BASE + 7.5,
                 op0=ALU.mult, op1=ALU.add,
             )
@@ -256,10 +256,9 @@ def tile_net_pa_kernel(tc, h1, coef2, sb2, sp2, b2, out):
                             in_=grouped.rearrange("p o t -> p (o t)"),
                         )
                 if piece == 1:
+                    find_cells(0)
                     for c in range(1, CHUNKS):
                         clip(c)
-                elif piece == O_PIECES - 1:
-                    for c in range(CHUNKS):
                         find_cells(c)
 
         def store(c, acc):

@@ -35,7 +35,7 @@ GPSIMD_FIRST_G = 11
 O_BLOCK = 22
 
 ROUND = 12582912.0
-CELL_BASE = 160.0
+MARK_BASE = 192.0
 V_HIGH = 20.0
 V_LOW = -104.0
 ROOT_THIRD = math.sqrt(1.0 / 3.0)
@@ -56,7 +56,9 @@ def words_on_partitions(matrix):
 def tile_net_pa_kernel(tc, h1, coef2, sb2, sp2, b2, out):
     nc = tc.nc
     with (
-        tc.manual_schedule(engines={mybir.EngineType.DVE, mybir.EngineType.Activation}),
+        tc.manual_schedule(
+            engines={mybir.EngineType.DVE, mybir.EngineType.Activation, mybir.EngineType.Pool}
+        ),
         tc.tile_pool(name="keep", bufs=1) as keep,
         tc.tile_pool(name="waves", bufs=2) as waves,
         tc.tile_pool(name="gates", bufs=2) as gates,
@@ -65,7 +67,6 @@ def tile_net_pa_kernel(tc, h1, coef2, sb2, sp2, b2, out):
     ):
         v = keep.tile([P, ALL], BF16, align_bytes=64)
         clipped = keep.tile([P, ALL], BF16)
-        cells = keep.tile([P, ALL], BF16)
         bias = keep.tile([P, OUTPUTS], BF16)
         w_codes = keep.tile([P, BRANCHES, OUTPUTS], U32, align_bytes=64)
         w_scales = keep.tile([P, BRANCHES, OUTPUTS], U8, align_bytes=64)
@@ -91,13 +92,6 @@ def tile_net_pa_kernel(tc, h1, coef2, sb2, sp2, b2, out):
             nc.scalar.activation(out=far[:, 1, :], in_=wave[:, 0, :], func=ACT.Abs, bias=-1.0)
             nc.scalar.activation(out=far[:, 0, :], in_=far[:, 1, :], func=ACT.Abs, scale=-1.0, bias=1.0)
             return from_8, wave, far
-
-        def find_cells(c):
-            part = slice(c * CHUNK, (c + 1) * CHUNK)
-            nc.vector.tensor_scalar(
-                out=cells[:, part], in0=clipped[:, part], scalar1=2.5, scalar2=CELL_BASE + 7.5,
-                op0=ALU.mult, op1=ALU.add,
-            )
 
         def mend_tiny(from_8, far):
             nc.vector.scalar_tensor_tensor(
@@ -200,9 +194,7 @@ def tile_net_pa_kernel(tc, h1, coef2, sb2, sp2, b2, out):
                 if in_group == 0:
                     group_width = len(group) * O_PIECE
                     w_grouped = early.tile([P, GPSIMD_FIRST_G, group_width, PACK], BF16, align_bytes=64)
-                    w_gpsimd = early.tile(
-                        [P, BASIS - GPSIMD_FIRST_G, group_width, PACK], BF16, align_bytes=64, bufs=2
-                    )
+                    w_gpsimd = early.tile([P, BASIS - GPSIMD_FIRST_G, group_width, PACK], BF16, align_bytes=64)
 
                 for g in range(GPSIMD_FIRST_G, BASIS):
                     nc.gpsimd.tensor_tensor(
@@ -242,6 +234,7 @@ def tile_net_pa_kernel(tc, h1, coef2, sb2, sp2, b2, out):
                         turn_h1(c)
                     slope = slope_of(wave)
                     gate = cube(0, far)
+                elif piece == 2:
                     nc.gpsimd.tensor_scalar(
                         out=base_grouped[:], in0=base_raw[:].rearrange("p t o -> p o t"), scalar1=1.0, scalar2=0.0,
                         op0=ALU.mult, op1=ALU.add,
@@ -256,10 +249,8 @@ def tile_net_pa_kernel(tc, h1, coef2, sb2, sp2, b2, out):
                             in_=grouped.rearrange("p o t -> p (o t)"),
                         )
                 if piece == 1:
-                    find_cells(0)
                     for c in range(1, CHUNKS):
                         clip(c)
-                        find_cells(c)
 
         def store(c, acc):
             for m in range(TILES_PER_CHUNK):
@@ -278,11 +269,11 @@ def tile_net_pa_kernel(tc, h1, coef2, sb2, sp2, b2, out):
                     out=chunk_slope[:], in0=chunk_wave[:], scalar=1.0, in1=chunk_slope[:], op0=ALU.subtract,
                     op1=ALU.mult,
                 )
-                quarter = basis.tile([P, COMBS, CHUNK], BF16)
+                mark = basis.tile([P, COMBS, CHUNK], BF16)
                 for r in range(COMBS):
                     nc.vector.tensor_scalar(
-                        out=quarter[:, r, :], in0=cells[:, c * CHUNK : (c + 1) * CHUNK], scalar1=0.25,
-                        scalar2=-(CELL_BASE + r + 1.5) / 4.0, op0=ALU.mult, op1=ALU.add,
+                        out=mark[:, r, :], in0=clipped[:, c * CHUNK : (c + 1) * CHUNK], scalar1=2.5 / 4.0,
+                        scalar2=MARK_BASE + (6.0 - r) / 4.0, op0=ALU.mult, op1=ALU.add,
                     )
                 periodic = basis.tile([P, COMBS, CHUNK], BF16)
                 nc.vector.scalar_tensor_tensor(
@@ -301,7 +292,7 @@ def tile_net_pa_kernel(tc, h1, coef2, sb2, sp2, b2, out):
                     count = combs_of[n]
                     inside = basis.tile([P, COMBS, CHUNK], BF16, bufs=2)
                     nc.vector.tensor_scalar(
-                        out=inside[:, 0:count, :], in0=quarter[:, 0:count, :], scalar1=ROUND, scalar2=ROUND + n,
+                        out=inside[:, 0:count, :], in0=mark[:, 0:count, :], scalar1=ROUND, scalar2=ROUND + MARK_BASE + n,
                         op0=ALU.add, op1=ALU.is_equal,
                     )
                     insides.append(inside)

@@ -30,7 +30,6 @@ ALL = CHUNKS * CHUNK
 
 O_PIECE = 128
 O_PIECES = OUTPUTS // O_PIECE
-O_GROUPS = ((0, 1), (2,), (3,))
 GPSIMD_FIRST_G = 11
 O_BLOCK = 22
 
@@ -57,7 +56,12 @@ def tile_net_pa_kernel(tc, h1, coef2, sb2, sp2, b2, out):
     nc = tc.nc
     with (
         tc.manual_schedule(
-            engines={mybir.EngineType.DVE, mybir.EngineType.Activation, mybir.EngineType.Pool}
+            engines={
+                mybir.EngineType.DVE,
+                mybir.EngineType.Activation,
+                mybir.EngineType.Pool,
+                mybir.EngineType.SP,
+            }
         ),
         tc.tile_pool(name="keep", bufs=1) as keep,
         tc.tile_pool(name="waves", bufs=2) as waves,
@@ -155,7 +159,6 @@ def tile_net_pa_kernel(tc, h1, coef2, sb2, sp2, b2, out):
             coef_pieces.append(load_coef(2, 1))
             for u in range(2):
                 nc.sync.dma_start(out=base_raw[:, 2 * u : 2 * u + 2, :], in_=words_on_partitions(sb2)[:, u])
-            nc.sync.dma_start(out=bias[:], in_=b2.partition_broadcast(P))
 
             identity = early.tile([P, P], F32)
             masks.make_identity(nc, identity[:])
@@ -188,19 +191,17 @@ def tile_net_pa_kernel(tc, h1, coef2, sb2, sp2, b2, out):
             from_8, wave, far = fold_waves(0)
             regroup_gain(0, O_PIECE)
 
-            for group, piece in [(group, piece) for group in O_GROUPS for piece in group]:
+            for piece in range(O_PIECES):
                 coef = coef_pieces[piece][:].rearrange("p t (o g) -> p t o g", g=BASIS)
-                in_group = (piece - group[0]) * O_PIECE
-                if in_group == 0:
-                    group_width = len(group) * O_PIECE
-                    w_grouped = early.tile([P, GPSIMD_FIRST_G, group_width, PACK], BF16, align_bytes=64)
-                    w_gpsimd = early.tile([P, BASIS - GPSIMD_FIRST_G, group_width, PACK], BF16, align_bytes=64)
+                columns = slice(piece * O_PIECE, (piece + 1) * O_PIECE)
+                w_grouped = early.tile([P, GPSIMD_FIRST_G, O_PIECE, PACK], BF16, align_bytes=64)
+                w_gpsimd = early.tile([P, BASIS - GPSIMD_FIRST_G, O_PIECE, PACK], BF16, align_bytes=64)
 
                 for g in range(GPSIMD_FIRST_G, BASIS):
                     nc.gpsimd.tensor_tensor(
-                        out=w_gpsimd[:, g - GPSIMD_FIRST_G, in_group : in_group + O_PIECE],
+                        out=w_gpsimd[:, g - GPSIMD_FIRST_G],
                         in0=coef[:, :, :, g].rearrange("p t o -> p o t"),
-                        in1=gain_grouped[:, piece * O_PIECE : (piece + 1) * O_PIECE],
+                        in1=gain_grouped[:, columns],
                         op=ALU.mult,
                     )
                 for o in range(0, O_PIECE, O_BLOCK):
@@ -216,7 +217,7 @@ def tile_net_pa_kernel(tc, h1, coef2, sb2, sp2, b2, out):
                         )
                     block_gain = gain_grouped[:, piece * O_PIECE + o : piece * O_PIECE + o + width]
                     nc.vector.tensor_tensor(
-                        out=w_grouped[:, :, in_group + o : in_group + o + width].rearrange("p g o t -> p g (o t)"),
+                        out=w_grouped[:, :, o : o + width].rearrange("p g o t -> p g (o t)"),
                         in0=bank[:].rearrange("p g o t -> p g (o t)"),
                         in1=block_gain.rearrange("p o t -> p (o t)")
                         .unsqueeze(1)
@@ -239,18 +240,17 @@ def tile_net_pa_kernel(tc, h1, coef2, sb2, sp2, b2, out):
                         out=base_grouped[:], in0=base_raw[:].rearrange("p t o -> p o t"), scalar1=1.0, scalar2=0.0,
                         op0=ALU.mult, op1=ALU.add,
                     )
-                if piece == group[-1]:
-                    columns = slice(group[0] * O_PIECE, (piece + 1) * O_PIECE)
-                    for g in range(BASIS):
-                        grouped = w_grouped[:, g] if g < GPSIMD_FIRST_G else w_gpsimd[:, g - GPSIMD_FIRST_G]
-                        nc.vector.quantize_mx(
-                            out=w_codes[:, g, columns].bitcast(FP8X4),
-                            scales=w_scales[:, g, columns],
-                            in_=grouped.rearrange("p o t -> p (o t)"),
-                        )
+                for g in range(BASIS):
+                    grouped = w_grouped[:, g] if g < GPSIMD_FIRST_G else w_gpsimd[:, g - GPSIMD_FIRST_G]
+                    nc.vector.quantize_mx(
+                        out=w_codes[:, g, columns].bitcast(FP8X4),
+                        scales=w_scales[:, g, columns],
+                        in_=grouped.rearrange("p o t -> p (o t)"),
+                    )
                 if piece == 1:
                     for c in range(1, CHUNKS):
                         clip(c)
+            nc.sync.dma_start(out=bias[:], in_=b2.partition_broadcast(P))
 
         def store(c, acc):
             for m in range(TILES_PER_CHUNK):

import math

import concourse.masks as masks
import concourse.mybir as mybir

F32 = mybir.dt.float32
BF16 = mybir.dt.bfloat16
U32 = mybir.dt.uint32
U8 = mybir.dt.uint8
FP8X4 = mybir.dt.float8_e4m3fn_x4
ALU = mybir.AluOpType
ACT = mybir.ActivationFunctionType

P = 128
PACK = 4
BATCH, FEATURES, OUTPUTS, BASIS = 1024, 512, 512, 13
BRANCHES = BASIS + 1
MISH = BASIS
FLOPS = 2 * BATCH * OUTPUTS * FEATURES * BRANCHES

COMBS = 4
WINDOWS = 4

ROW_TILES = BATCH // P
TILES_PER_CHUNK = 2
CHUNKS = ROW_TILES // TILES_PER_CHUNK
CHUNK_WORDS = TILES_PER_CHUNK * P
CHUNK = CHUNK_WORDS * PACK
ALL = CHUNKS * CHUNK

O_PIECE = 128
O_PIECES = OUTPUTS // O_PIECE
GPSIMD_FIRST_G = 11
O_BLOCK = 22

ROUND = 12582912.0
MARK_BASE = 192.0
V_HIGH = 20.0
V_LOW = -104.0
ROOT_THIRD = math.sqrt(1.0 / 3.0)
LOG_SIXTH = math.log(1.0 / 6.0)
NEAREST = 2.0**-10
SPECK = 2.0**-60


def half_of_features(matrix, u):
    half = FEATURES // 2
    return matrix[u * half : (u + 1) * half]


def words_on_partitions(matrix):
    return matrix.rearrange("(u p e) n -> p u e n", u=2, e=2)


def tile_net_pa_kernel(tc, h1, coef2, sb2, sp2, b2, out):
    nc = tc.nc
    with (
        tc.manual_schedule(
            engines={
                mybir.EngineType.DVE,
                mybir.EngineType.Activation,
                mybir.EngineType.Pool,
                mybir.EngineType.SP,
            }
        ),
        tc.tile_pool(name="keep", bufs=1) as keep,
        tc.tile_pool(name="waves", bufs=2) as waves,
        tc.tile_pool(name="gates", bufs=2) as gates,
        tc.tile_pool(name="ring", bufs=2) as ring,
        tc.psum_pool(name="psum", bufs=2) as psum,
    ):
        v = keep.tile([P, ALL], BF16, align_bytes=64)
        clipped = keep.tile([P, ALL], BF16)
        bias = keep.tile([P, OUTPUTS], BF16)
        w_codes = keep.tile([P, BRANCHES, OUTPUTS], U32, align_bytes=64)
        w_scales = keep.tile([P, BRANCHES, OUTPUTS], U8, align_bytes=64)
        base_raw = keep.tile([P, PACK, OUTPUTS], BF16)
        base_grouped = keep.tile([P, OUTPUTS, PACK], BF16, align_bytes=64)

        def clip(c):
            part = slice(c * CHUNK, (c + 1) * CHUNK)
            nc.vector.tensor_scalar(
                out=clipped[:, part], in0=v[:, part], scalar1=V_LOW, scalar2=V_HIGH, op0=ALU.max, op1=ALU.min
            )

        def fold_waves(c):
            chunk = clipped[:, c * CHUNK : (c + 1) * CHUNK]
            from_8 = waves.tile([P, CHUNK], F32, bufs=1)
            wave = waves.tile([P, 2, CHUNK], F32)
            nc.scalar.activation(out=from_8[:], in_=chunk, func=ACT.Abs, scale=2.5)
            nc.scalar.activation(out=wave[:, 0, :], in_=from_8[:], func=ACT.Abs, bias=-4.0)
            nc.scalar.activation(out=wave[:, 1, :], in_=chunk, func=ACT.Abs, scale=2.5, bias=-1.0)
            nc.scalar.activation(out=wave[:, 1, :], in_=wave[:, 1, :], func=ACT.Abs, bias=-4.0)
            nc.scalar.activation(out=wave[:], in_=wave[:], func=ACT.Abs, bias=-2.0)
            far = waves.tile([P, 2, CHUNK], F32)
            nc.scalar.activation(out=far[:, 1, :], in_=wave[:, 0, :], func=ACT.Abs, bias=-1.0)
            nc.scalar.activation(out=far[:, 0, :], in_=far[:, 1, :], func=ACT.Abs, scale=-1.0, bias=1.0)
            return from_8, wave, far

        def mend_tiny(from_8, far):
            nc.vector.scalar_tensor_tensor(
                out=far[:, 0, :], in0=far[:, 0, :], scalar=NEAREST, in1=from_8[:], op0=ALU.max, op1=ALU.min
            )

        def slope_of(wave):
            slope = waves.tile([P, 2, CHUNK], F32)
            nc.scalar.activation(out=slope[:], in_=wave[:], func=ACT.Square, scale=ROOT_THIRD, bias=-ROOT_THIRD)
            nc.scalar.activation(out=slope[:], in_=slope[:], func=ACT.Identity, scale=-1.0, bias=1.0)
            return slope

        def cube(c, far):
            gate = gates.tile([P, CHUNK], F32)
            nc.scalar.activation(out=gate[:], in_=clipped[:, c * CHUNK : (c + 1) * CHUNK], func=ACT.Exp)
            nc.scalar.activation(out=far[:], in_=far[:], func=ACT.Ln, bias=SPECK)
            nc.scalar.activation(out=gate[:], in_=gate[:], func=ACT.Ln, bias=1.0)
            nc.scalar.activation(out=far[:], in_=far[:], func=ACT.Exp, scale=3.0, bias=LOG_SIXTH)
            nc.scalar.activation(out=gate[:], in_=gate[:], func=ACT.Tanh)
            return gate

        with (
            tc.tile_pool(name="early", bufs=1) as early,
            tc.tile_pool(name="stream", bufs=3) as stream,
        ):
            h1_rows = early.tile([P, ROW_TILES, FEATURES], BF16)
            h1_by_tile = h1.rearrange("(m p) i -> p m i", p=P)
            gain = early.tile([P, PACK, OUTPUTS], BF16)

            def load_h1(c):
                tiles = slice(c * TILES_PER_CHUNK, (c + 1) * TILES_PER_CHUNK)
                nc.sync.dma_start(out=h1_rows[:, tiles, :], in_=h1_by_tile[:, tiles, :])

            def load_gain(first, last):
                for u in range(2):
                    nc.sync.dma_start(
                        out=gain[:, 2 * u : 2 * u + 2, first:last], in_=words_on_partitions(sp2)[:, u, :, first:last]
                    )

            def load_coef(piece, parts):
                coef_raw = stream.tile([P, PACK, O_PIECE * BASIS], BF16)
                width = O_PIECE // parts
                for part in range(parts):
                    for u in range(2):
                        first = piece * O_PIECE + part * width
                        nc.sync.dma_start(
                            out=coef_raw[:, 2 * u : 2 * u + 2, part * width * BASIS : (part + 1) * width * BASIS],
                            in_=half_of_features(coef2, u)[:, first : first + width, :].rearrange(
                                "(p e) o g -> p e (o g)", e=2
                            ),
                        )
                return coef_raw

            load_h1(0)
            load_gain(0, O_PIECE)
            coef_pieces = [load_coef(0, 2)]
            load_gain(O_PIECE, OUTPUTS)
            coef_pieces.append(load_coef(1, 1))
            for c in range(1, CHUNKS):
                load_h1(c)
            coef_pieces.append(load_coef(2, 1))
            for u in range(2):
                nc.sync.dma_start(out=base_raw[:, 2 * u : 2 * u + 2, :], in_=words_on_partitions(sb2)[:, u])

            identity = early.tile([P, P], F32)
            masks.make_identity(nc, identity[:])
            identity_bf = early.tile([P, P], BF16)
            masks.make_identity(nc, identity_bf[:])

            h1_words = h1_rows[:].bitcast(F32)
            v_words = v[:].bitcast(F32).rearrange("p (c m b u) -> p c m b u", c=CHUNKS, m=TILES_PER_CHUNK, u=2)

            def turn_h1(c):
                turned = psum.tile([P, TILES_PER_CHUNK, 2, P], F32, tag="turn", bufs=4)
                for m in range(TILES_PER_CHUNK):
                    for u in range(2):
                        nc.tensor.transpose(
                            out=turned[:, m, u, :],
                            in_=h1_words[:, c * TILES_PER_CHUNK + m, u * P : (u + 1) * P],
                            identity=identity[:],
                        )
                nc.scalar.copy(out=v_words[:, c], in_=turned[:].rearrange("p m u b -> p m b u"))

            gain_grouped = early.tile([P, OUTPUTS, PACK], BF16)

            def regroup_gain(first, last):
                nc.vector.tensor_copy(
                    out=gain_grouped[:, first:last], in_=gain[:, :, first:last].rearrange("p t o -> p o t")
                )

            turn_h1(0)
            clip(0)
            from_8, wave, far = fold_waves(0)
            regroup_gain(0, O_PIECE)

            for piece in range(O_PIECES):
                coef = coef_pieces[piece][:].rearrange("p t (o g) -> p t o g", g=BASIS)
                columns = slice(piece * O_PIECE, (piece + 1) * O_PIECE)
                w_grouped = early.tile([P, GPSIMD_FIRST_G, O_PIECE, PACK], BF16, align_bytes=64)
                w_gpsimd = early.tile([P, BASIS - GPSIMD_FIRST_G, O_PIECE, PACK], BF16, align_bytes=64)

                for g in range(GPSIMD_FIRST_G, BASIS):
                    nc.gpsimd.tensor_tensor(
                        out=w_gpsimd[:, g - GPSIMD_FIRST_G],
                        in0=coef[:, :, :, g].rearrange("p t o -> p o t"),
                        in1=gain_grouped[:, columns],
                        op=ALU.mult,
                    )
                for o in range(0, O_PIECE, O_BLOCK):
                    width = min(O_BLOCK, O_PIECE - o)
                    bank = psum.tile([P, GPSIMD_FIRST_G, width, PACK], BF16, tag="turn", bufs=4)
                    for u in range(2):
                        nc.tensor.matmul(
                            out=bank[:, :, :, 2 * u : 2 * u + 2].rearrange("p g o e -> p e o g"),
                            lhsT=identity_bf[:],
                            rhs=coef[:, 2 * u : 2 * u + 2, o : o + width, 0:GPSIMD_FIRST_G],
                            start=True,
                            stop=True,
                        )
                    block_gain = gain_grouped[:, piece * O_PIECE + o : piece * O_PIECE + o + width]
                    nc.vector.tensor_tensor(
                        out=w_grouped[:, :, o : o + width].rearrange("p g o t -> p g (o t)"),
                        in0=bank[:].rearrange("p g o t -> p g (o t)"),
                        in1=block_gain.rearrange("p o t -> p (o t)")
                        .unsqueeze(1)
                        .to_broadcast([P, GPSIMD_FIRST_G, width * PACK]),
                        op=ALU.mult,
                    )
                if piece + 3 < O_PIECES:
                    coef_pieces.append(load_coef(piece + 3, 1))

                if piece == 0:
                    regroup_gain(O_PIECE, OUTPUTS)
                elif piece == 1:
                    mend_tiny(from_8, far)
                    for c in range(1, CHUNKS):
                        turn_h1(c)
                    slope = slope_of(wave)
                    gate = cube(0, far)
                elif piece == 2:
                    nc.gpsimd.tensor_scalar(
                        out=base_grouped[:], in0=base_raw[:].rearrange("p t o -> p o t"), scalar1=1.0, scalar2=0.0,
                        op0=ALU.mult, op1=ALU.add,
                    )
                for g in range(BASIS):
                    grouped = w_grouped[:, g] if g < GPSIMD_FIRST_G else w_gpsimd[:, g - GPSIMD_FIRST_G]
                    nc.vector.quantize_mx(
                        out=w_codes[:, g, columns].bitcast(FP8X4),
                        scales=w_scales[:, g, columns],
                        in_=grouped.rearrange("p o t -> p (o t)"),
                    )
                if piece == 1:
                    for c in range(1, CHUNKS):
                        clip(c)
            nc.sync.dma_start(out=bias[:], in_=b2.partition_broadcast(P))

        def store(c, acc):
            for m in range(TILES_PER_CHUNK):
                result = ring.tile([P, OUTPUTS], F32)
                nc.vector.tensor_tensor(out=result[:], in0=acc[m][:], in1=bias[:], op=ALU.add)
                row0 = (c * TILES_PER_CHUNK + m) * P
                nc.sync.dma_start(out=out[row0 : row0 + P, :], in_=result[:])

        acc = None
        next_fold = fold_waves(1)
        with tc.tile_pool(name="basis", bufs=1) as basis:
            for c in range(CHUNKS):
                chunk_wave, chunk_far, chunk_slope, chunk_gate = wave, far, slope, gate

                nc.vector.scalar_tensor_tensor(
                    out=chunk_slope[:], in0=chunk_wave[:], scalar=1.0, in1=chunk_slope[:], op0=ALU.subtract,
                    op1=ALU.mult,
                )
                mark = basis.tile([P, COMBS, CHUNK], BF16)
                for r in range(COMBS):
                    nc.vector.tensor_scalar(
                        out=mark[:, r, :], in0=clipped[:, c * CHUNK : (c + 1) * CHUNK], scalar1=2.5 / 4.0,
                        scalar2=MARK_BASE + (6.0 - r) / 4.0, op0=ALU.mult, op1=ALU.add,
                    )
                periodic = basis.tile([P, COMBS, CHUNK], BF16)
                nc.vector.scalar_tensor_tensor(
                    out=periodic[:, 0:2, :], in0=chunk_slope[:], scalar=0.0, in1=chunk_far[:], op0=ALU.min,
                    op1=ALU.subtract, reverse1=True,
                )
                nc.vector.scalar_tensor_tensor(
                    out=periodic[:, 2:4, :], in0=chunk_slope[:], scalar=0.0, in1=chunk_far[:], op0=ALU.max, op1=ALU.add
                )

                combs_of = [sum(1 for r in range(COMBS) if r + COMBS * n < BASIS) for n in range(WINDOWS)]
                insides = []
                slabs = []

                def find_window(n):
                    count = combs_of[n]
                    inside = basis.tile([P, COMBS, CHUNK], BF16, bufs=2)
                    nc.vector.tensor_scalar(
                        out=inside[:, 0:count, :], in0=mark[:, 0:count, :], scalar1=ROUND, scalar2=ROUND + MARK_BASE + n,
                        op0=ALU.add, op1=ALU.is_equal,
                    )
                    insides.append(inside)

                def cut_out(n):
                    count = combs_of[n]
                    slab = basis.tile([P, COMBS, CHUNK], BF16, align_bytes=64, bufs=2)
                    nc.vector.tensor_tensor(
                        out=slab[:, 0:count, :], in0=periodic[:, 0:count, :], in1=insides[n][:, 0:count, :], op=ALU.mult
                    )
                    slabs.append(slab)

                def multiply(codes, scales, branch, first, last):
                    for m in range(TILES_PER_CHUNK):
                        rows = slice(m * P, (m + 1) * P)
                        nc.tensor.matmul_mx(
                            out=acc[m][:],
                            lhsT=codes[:, rows].bitcast(FP8X4),
                            lhsT_scale=scales[:, rows],
                            rhs=w_codes[:, branch, :].bitcast(FP8X4),
                            rhs_scale=w_scales[:, branch, :],
                            start=first,
                            stop=last,
                        )

                def quantise_and_multiply(n):
                    count = combs_of[n]
                    codes = ring.tile([P, COMBS, CHUNK_WORDS], U32, align_bytes=64)
                    scales = ring.tile([P, COMBS, CHUNK_WORDS], U8, align_bytes=64)
                    nc.vector.quantize_mx(
                        out=codes[:, 0:count, :].rearrange("p r w -> p (r w)").bitcast(FP8X4),
                        scales=scales[:, 0:count, :].rearrange("p r w -> p (r w)"),
                        in_=slabs[n][:, 0:count, :].rearrange("p r k -> p (r k)"),
                    )
                    for r in range(count):
                        g = r + COMBS * n
                        multiply(codes[:, r, :], scales[:, r, :], g, g == 0, g == BASIS - 1)

                find_window(0)
                if c == 0:
                    nc.vector.quantize_mx(
                        out=w_codes[:, MISH, :].bitcast(FP8X4),
                        scales=w_scales[:, MISH, :],
                        in_=base_grouped[:].rearrange("p o t -> p (o t)"),
                    )
                last_acc = acc
                acc = [
                    psum.tile([P, OUTPUTS], F32, name="acc", bufs=2 * TILES_PER_CHUNK)
                    for m in range(TILES_PER_CHUNK)
                ]
                find_window(1)
                cut_out(0)
                if c + 1 < CHUNKS:
                    from_8, wave, far = next_fold
                    mend_tiny(from_8, far)
                    slope = slope_of(wave)
                    gate = cube(c + 1, far)
                if c + 2 < CHUNKS:
                    next_fold = fold_waves(c + 2)
                quantise_and_multiply(0)
                for n in range(1, WINDOWS - 1):
                    cut_out(n)
                    find_window(n + 1)
                    quantise_and_multiply(n)
                mish = gates.tile([P, CHUNK], BF16, align_bytes=64)
                nc.vector.tensor_tensor(
                    out=mish[:], in0=v[:, c * CHUNK : (c + 1) * CHUNK], in1=chunk_gate[:], op=ALU.mult
                )
                if c > 0:
                    store(c - 1, last_acc)
                cut_out(WINDOWS - 1)
                mish_codes = ring.tile([P, CHUNK_WORDS], U32, align_bytes=64)
                mish_scales = ring.tile([P, CHUNK_WORDS], U8, align_bytes=64)
                nc.vector.quantize_mx(out=mish_codes[:].bitcast(FP8X4), scales=mish_scales[:], in_=mish[:])
                multiply(mish_codes, mish_scales, MISH, False, False)
                quantise_and_multiply(WINDOWS - 1)
            store(CHUNKS - 1, acc)
